import numpy as np
import ml_dtypes


def mxq(x, axis, fmt="e4m3"):
    dtype, down = {"e4m3": (ml_dtypes.float8_e4m3fn, 7), "e5m2": (ml_dtypes.float8_e5m2, 14)}[fmt]
    v = np.moveaxis(np.asarray(x, np.float32).astype(ml_dtypes.bfloat16).astype(np.float64), axis, -1)
    blocks = v.reshape(v.shape[:-1] + (-1, 32))
    amax = np.abs(blocks).max(-1, keepdims=True)
    byte = np.maximum(np.where(amax > 0, np.frexp(amax)[1] - 1 + 127, 0) - down, 1)
    scale = np.exp2(byte - 127.0)
    codes = (blocks / scale).astype(np.float32).astype(dtype).astype(np.float64)
    return np.moveaxis((codes * scale).reshape(v.shape), -1, axis)


WIDE = False


def mx_kscale(k):
    if not WIDE:
        return np.ones(k)
    levels = np.array([30, -30])
    if k % 512:
        return np.exp2(np.random.permutation(np.resize(levels, k // 32))).repeat(32)
    a = np.empty((k // 512, 16))
    for p in range(k // 512):
        a[p, :8] = np.random.permutation(np.resize(levels, 8))
        for g in range(8):
            far = levels[np.abs(levels - a[p, g]) >= 10]
            a[p, g + 8] = far[np.random.randint(len(far))]
    return np.exp2(a.ravel()).repeat(32)


BF16 = ml_dtypes.bfloat16


def bf(x):
    return np.asarray(x, np.float32).astype(BF16)


def f64(x):
    return np.asarray(x).astype(np.float64)


B, LP, LE, H, KV, D, DH, DE = 2, 256, 256, 8, 4, 256, 2048, 1024
L = LP + LE
DHALF = D // 2


def rope(x, cos, sin):
    x1, x2 = x[..., :DHALF], x[..., DHALF:]
    return np.concatenate([x1 * cos - x2 * sin, x2 * cos + x1 * sin], axis=-1)


def setup_inputs():
    s0, s1 = mx_kscale(DH), mx_kscale(DE)
    pos = np.arange(L, dtype=np.float64)
    inv_freq = 1.0 / (10000.0 ** (np.arange(0, DHALF, dtype=np.float64) / DHALF))
    ang = pos[:, None] * inv_freq[None, :]
    return {"pg_embeds": bf(np.random.standard_normal((B, LP, DH)) * s0),
            "exp_embeds": bf(np.random.standard_normal((B, LE, DE)) * s1),
            "cos": bf(np.cos(ang)[None, :, None, :]),
            "sin": bf(np.sin(ang)[None, :, None, :]),
            "wq0": bf(np.random.standard_normal((H * D, DH)) * 1.25 / np.sqrt(DH) / s0[None, :]),
            "wk0": bf(np.random.standard_normal((KV * D, DH)) * 1.25 / np.sqrt(DH) / s0[None, :]),
            "wq1": bf(np.random.standard_normal((H * D, DE)) * 1.25 / np.sqrt(DE) / s1[None, :]),
            "wk1": bf(np.random.standard_normal((KV * D, DE)) * 1.25 / np.sqrt(DE) / s1[None, :])}


def reference(pg_embeds, exp_embeds, cos, sin, wq0, wk0, wq1, wk1):
    xp = mxq(f64(pg_embeds), 2, "e5m2")
    xe = mxq(f64(exp_embeds), 2, "e5m2")
    q = np.concatenate([
        (xp @ mxq(f64(wq0), 1, "e5m2").T).reshape(B, LP, H, D),
        (xe @ mxq(f64(wq1), 1, "e5m2").T).reshape(B, LE, H, D)], axis=1)
    k = np.concatenate([
        (xp @ mxq(f64(wk0), 1, "e5m2").T).reshape(B, LP, KV, D),
        (xe @ mxq(f64(wk1), 1, "e5m2").T).reshape(B, LE, KV, D)], axis=1)
    c, s = f64(cos), f64(sin)
    return rope(q, c, s), rope(k, c, s)

@@ -1,0 +1,178 @@
+from contextlib import ExitStack
+
+import concourse.mybir as mybir
+from concourse.masks import make_identity
+
+F32 = mybir.dt.float32
+BF16 = mybir.dt.bfloat16
+U32 = mybir.dt.uint32
+U8 = mybir.dt.uint8
+E5X4 = mybir.dt.float8_e5m2_x4
+MULT = mybir.AluOpType.mult
+ADD = mybir.AluOpType.add
+SUB = mybir.AluOpType.subtract
+
+FLOPS = 2 * 512 * 3072 * (2048 + 1024)
+
+P = 128
+RAW_BUFS = 10
+
+
+def tile_paligemma2withexpertmodel_pa_kernel(
+    tc, pg_embeds, exp_embeds, cos, sin, wq0, wk0, wq1, wk1, out_0, out_1
+):
+    nc = tc.nc
+    xsrc = {"p": pg_embeds.flatten_outer_dims(), "e": exp_embeds.flatten_outer_dims()}
+    wsrc = {"p": (wq0, wk0), "e": (wq1, wk1)}
+    halves = {"p": 2, "e": 1}
+
+    def x_view(st, kh):
+        return xsrc[st][:, kh * 1024 : (kh + 1) * 1024].rearrange("(m p) k -> p m k", p=P)
+
+    def w_view(st, s, f, kh):
+        w = wsrc[st][0] if s < 2 else wsrc[st][1]
+        r0 = 1024 * (s % 2)
+        v = w[r0 : r0 + 1024, kh * 1024 : (kh + 1) * 1024]
+        return v.rearrange("(h f p) k -> f p h k", f=2, p=P)[f]
+
+    def x_jobs(st):
+        return [(("x", st, kh), x_view(st, kh)) for kh in range(halves[st])]
+
+    def w_jobs(st, s):
+        return [
+            (("w", st, s, f, kh), w_view(st, s, f, kh))
+            for f in range(2)
+            for kh in range(halves[st])
+        ]
+
+    tjobs = (
+        x_jobs("e") + w_jobs("e", 0) + w_jobs("e", 1) + x_jobs("p") + w_jobs("p", 0)
+        + w_jobs("e", 2) + w_jobs("p", 1) + w_jobs("p", 2)
+    )
+    units = [
+        (st, s, m)
+        for (st, s) in (("e", 0), ("e", 1), ("p", 0), ("e", 2), ("p", 1), ("p", 2))
+        for m in range(4)
+    ]
+
+    with ExitStack() as ctx:
+        ctx.enter_context(tc.manual_schedule())
+        const = ctx.enter_context(tc.tile_pool(name="const", bufs=1))
+        rawp = ctx.enter_context(tc.tile_pool(name="rawp", bufs=RAW_BUFS))
+        grp = ctx.enter_context(tc.tile_pool(name="grp", bufs=3))
+        wcp = ctx.enter_context(tc.tile_pool(name="wcp", bufs=8))
+        xcp = ctx.enter_context(tc.tile_pool(name="xcp", bufs=1))
+        ropep = ctx.enter_context(tc.tile_pool(name="ropep", bufs=3))
+        outp = ctx.enter_context(tc.tile_pool(name="outp", bufs=4))
+        tpp = ctx.enter_context(tc.psum_pool(name="tpp", bufs=4))
+        accp = ctx.enter_context(tc.psum_pool(name="accp", bufs=2))
+
+        ident = const.tile([P, P], F32, name="ident", tag="ident")
+        make_identity(nc, ident[:])
+        cos_t = const.tile([P, 4, P], BF16, name="cos_t", tag="cos_t")
+        sin_t = const.tile([P, 4, P], BF16, name="sin_t", tag="sin_t")
+
+        raws = {}
+        codes = {}
+
+        def load(n):
+            raw = rawp.tile([P, 4, 1024], BF16, name="raw%d" % n, tag="raw")
+            nc.sync.dma_start(out=raw[:], in_=tjobs[n][1])
+            raws[n] = raw
+
+        def tjob(j):
+            key = tjobs[j][0]
+            words = raws[j][:].rearrange("p i k -> p (i k)").bitcast(F32)
+            grouped = grp.tile([P, 1024, 4], BF16, name="grouped%d" % j, tag="grouped", align_bytes=64)
+            for b in range(4):
+                tp = tpp.tile([P, 2, 256], F32, name="tp%d_%d" % (j, b), tag="tp")
+                for il in range(2):
+                    off = (2 * (b % 2) + il) * 512 + (b // 2) * 256
+                    for u in range(2):
+                        nc.tensor.transpose(
+                            tp[:, u, il * P : (il + 1) * P],
+                            words[:, off + u : off + 256 : 2],
+                            ident[:],
+                        )
+                nc.scalar.copy(
+                    out=grouped[:, 256 * b : 256 * (b + 1), :].bitcast(F32),
+                    in_=tp[:].rearrange("p u c -> p c u"),
+                )
+            if key[0] == "x":
+                cd = xcp.tile([P, 1024], U32, name="xc%d" % j, tag="xc%d" % j, align_bytes=64)
+                sc = xcp.tile([P, 1024], U8, name="xs%d" % j, tag="xs%d" % j, align_bytes=64)
+            else:
+                cd = wcp.tile([P, 1024], U32, name="wc%d" % j, tag="wc", align_bytes=64)
+                sc = wcp.tile([P, 1024], U8, name="ws%d" % j, tag="ws", align_bytes=64)
+            nc.vector.quantize_mx(
+                out=cd[:].bitcast(E5X4),
+                scales=sc[:],
+                in_=grouped[:].rearrange("p c t -> p (c t)"),
+            )
+            codes[key] = (cd, sc)
+
+        def unit(n):
+            st, s, m = units[n]
+            npass = 2 * halves[st]
+            accs = []
+            for f in range(2):
+                acc = accp.tile([P, 512], F32, name="acc%d_%d" % (n, f), tag="acc%d" % f)
+                for g in range(npass):
+                    xc, xs = codes[("x", st, g // 2)]
+                    wc, ws = codes[("w", st, s, f, g // 2)]
+                    c0 = (g % 2) * 512
+                    nc.tensor.matmul_mx(
+                        out=acc[:],
+                        lhsT=xc[:, c0 + m * P : c0 + (m + 1) * P].bitcast(E5X4),
+                        lhsT_scale=xs[:, c0 + m * P : c0 + (m + 1) * P],
+                        rhs=wc[:, c0 : c0 + 512].bitcast(E5X4),
+                        rhs_scale=ws[:, c0 : c0 + 512],
+                        start=(g == 0),
+                        stop=(g == npass - 1),
+                    )
+                accs.append(acc[:].rearrange("p (h d) -> p h d", h=4))
+            pt = (m % 2) + (0 if st == "p" else 2)
+            cb = cos_t[:, pt, :].unsqueeze(1).to_broadcast([P, 4, P])
+            sb = sin_t[:, pt, :].unsqueeze(1).to_broadcast([P, 4, P])
+            t_c = ropep.tile([P, 2, 4, P], F32, name="t_c%d" % n, tag="t_c")
+            t_s = ropep.tile([P, 2, 4, P], F32, name="t_s%d" % n, tag="t_s")
+            nc.vector.tensor_tensor(out=t_c[:, 0], in0=accs[0], in1=cb, op=MULT)
+            nc.vector.tensor_tensor(out=t_s[:, 1], in0=accs[0], in1=sb, op=MULT)
+            nc.vector.tensor_tensor(out=t_s[:, 0], in0=accs[1], in1=sb, op=MULT)
+            nc.vector.tensor_tensor(out=t_c[:, 1], in0=accs[1], in1=cb, op=MULT)
+            o = outp.tile([P, 4, 2, P], F32, name="o%d" % n, tag="o")
+            nc.gpsimd.tensor_tensor(out=o[:, :, 0, :], in0=t_c[:, 0], in1=t_s[:, 0], op=SUB)
+            nc.gpsimd.tensor_tensor(out=o[:, :, 1, :], in0=t_c[:, 1], in1=t_s[:, 1], op=ADD)
+            b = m // 2
+            rows = slice(pt * P, (pt + 1) * P)
+            if s < 2:
+                dst = out_0[b, rows, 4 * s : 4 * s + 4, :]
+            else:
+                dst = out_1[b, rows, :, :]
+            nc.sync.dma_start(
+                out=dst.rearrange("p h d -> p (h d)"),
+                in_=o[:].rearrange("p h f d -> p (h f d)"),
+            )
+
+        for n in range(3):
+            load(n)
+        nc.sync.dma_start(out=cos_t[:], in_=cos[0, :, 0, :].rearrange("(t p) d -> p t d", p=P))
+        nc.sync.dma_start(out=sin_t[:], in_=sin[0, :, 0, :].rearrange("(t p) d -> p t d", p=P))
+        for n in range(3, RAW_BUFS):
+            load(n)
+
+        done = 0
+        issued = 0
+        for j in range(len(tjobs)):
+            tjob(j)
+            if j + RAW_BUFS < len(tjobs):
+                load(j + RAW_BUFS)
+            if j < 3:
+                continue
+            quota = 4 * (j - 2) if j <= 10 else 32 + 8 * (j - 10)
+            if j == len(tjobs) - 1:
+                quota = 144
+            while done < len(units) and issued < quota:
+                issued += 4 * halves[units[done][0]]
+                unit(done)
+                done += 1

@@ -16,6 +16,8 @@ FLOPS = 2 * 512 * 3072 * (2048 + 1024)
 
 P = 128
 RAW_BUFS = 10
+WARM_FIRST = 10
+HEAD_JOBS = 4
 
 
 def tile_paligemma2withexpertmodel_pa_kernel(
@@ -72,8 +74,16 @@ def tile_paligemma2withexpertmodel_pa_kernel(
         cos_t = const.tile([P, 4, P], BF16, name="cos_t", tag="cos_t")
         sin_t = const.tile([P, 4, P], BF16, name="sin_t", tag="sin_t")
 
+        zeros = const.tile([P, 512], BF16, name="zeros", tag="zeros")
+        nc.vector.memset(zeros[:], 0.0)
+
         raws = {}
         codes = {}
+
+        def warm(count, name):
+            scrap = accp.tile([P, 512], F32, name=name, tag="acc0")
+            for i in range(count):
+                nc.tensor.matmul(scrap[:], lhsT=zeros[:, 0:P], rhs=zeros[:], start=True, stop=True)
 
         def load(n):
             raw = rawp.tile([P, 4, 1024], BF16, name="raw%d" % n, tag="raw")
@@ -98,6 +108,8 @@ def tile_paligemma2withexpertmodel_pa_kernel(
                     out=grouped[:, 256 * b : 256 * (b + 1), :].bitcast(F32),
                     in_=tp[:].rearrange("p u c -> p c u"),
                 )
+                if j < HEAD_JOBS and b % 2 == 1:
+                    warm(2, "scrap%d_%d" % (j, b))
             if key[0] == "x":
                 cd = xcp.tile([P, 1024], U32, name="xc%d" % j, tag="xc%d" % j, align_bytes=64)
                 sc = xcp.tile([P, 1024], U8, name="xs%d" % j, tag="xs%d" % j, align_bytes=64)
@@ -138,11 +150,12 @@ def tile_paligemma2withexpertmodel_pa_kernel(
             t_s = ropep.tile([P, 2, 4, P], F32, name="t_s%d" % n, tag="t_s")
             nc.vector.tensor_tensor(out=t_c[:, 0], in0=accs[0], in1=cb, op=MULT)
             nc.vector.tensor_tensor(out=t_s[:, 1], in0=accs[0], in1=sb, op=MULT)
-            nc.vector.tensor_tensor(out=t_s[:, 0], in0=accs[1], in1=sb, op=MULT)
             nc.vector.tensor_tensor(out=t_c[:, 1], in0=accs[1], in1=cb, op=MULT)
+            nc.vector.tensor_tensor(out=t_s[:, 0], in0=accs[1], in1=sb, op=MULT)
             o = outp.tile([P, 4, 2, P], F32, name="o%d" % n, tag="o")
-            nc.gpsimd.tensor_tensor(out=o[:, :, 0, :], in0=t_c[:, 0], in1=t_s[:, 0], op=SUB)
-            nc.gpsimd.tensor_tensor(out=o[:, :, 1, :], in0=t_c[:, 1], in1=t_s[:, 1], op=ADD)
+            adder = nc.vector if n == len(units) - 1 else nc.gpsimd
+            adder.tensor_tensor(out=o[:, :, 0, :], in0=t_c[:, 0], in1=t_s[:, 0], op=SUB)
+            adder.tensor_tensor(out=o[:, :, 1, :], in0=t_c[:, 1], in1=t_s[:, 1], op=ADD)
             b = m // 2
             rows = slice(pt * P, (pt + 1) * P)
             if s < 2:
@@ -154,12 +167,13 @@ def tile_paligemma2withexpertmodel_pa_kernel(
                 in_=o[:].rearrange("p h f d -> p (h f d)"),
             )
 
-        for n in range(3):
+        for n in range(5):
             load(n)
         nc.sync.dma_start(out=cos_t[:], in_=cos[0, :, 0, :].rearrange("(t p) d -> p t d", p=P))
         nc.sync.dma_start(out=sin_t[:], in_=sin[0, :, 0, :].rearrange("(t p) d -> p t d", p=P))
-        for n in range(3, RAW_BUFS):
+        for n in range(5, RAW_BUFS):
             load(n)
+        warm(WARM_FIRST, "scrap_first")
 
         done = 0
         issued = 0

@@ -17,7 +17,8 @@ FLOPS = 2 * 512 * 3072 * (2048 + 1024)
 P = 128
 RAW_BUFS = 10
 WARM_FIRST = 10
-HEAD_JOBS = 4
+FIRST_SORTED_JOB = 11
+SORTED_PIECES = 3
 
 
 def tile_paligemma2withexpertmodel_pa_kernel(
@@ -62,10 +63,11 @@ def tile_paligemma2withexpertmodel_pa_kernel(
         const = ctx.enter_context(tc.tile_pool(name="const", bufs=1))
         rawp = ctx.enter_context(tc.tile_pool(name="rawp", bufs=RAW_BUFS))
         grp = ctx.enter_context(tc.tile_pool(name="grp", bufs=3))
+        srt = ctx.enter_context(tc.tile_pool(name="srt", bufs=3))
         wcp = ctx.enter_context(tc.tile_pool(name="wcp", bufs=8))
         xcp = ctx.enter_context(tc.tile_pool(name="xcp", bufs=1))
         ropep = ctx.enter_context(tc.tile_pool(name="ropep", bufs=3))
-        outp = ctx.enter_context(tc.tile_pool(name="outp", bufs=4))
+        outp = ctx.enter_context(tc.tile_pool(name="outp", bufs=6))
         tpp = ctx.enter_context(tc.psum_pool(name="tpp", bufs=4))
         accp = ctx.enter_context(tc.psum_pool(name="accp", bufs=2))
 
@@ -78,6 +80,7 @@ def tile_paligemma2withexpertmodel_pa_kernel(
         nc.vector.memset(zeros[:], 0.0)
 
         raws = {}
+        sorted_words = {}
         codes = {}
 
         def warm(count, name):
@@ -90,6 +93,18 @@ def tile_paligemma2withexpertmodel_pa_kernel(
             nc.sync.dma_start(out=raw[:], in_=tjobs[n][1])
             raws[n] = raw
 
+        def sort_words(j):
+            if j < FIRST_SORTED_JOB or j >= len(tjobs):
+                return
+            n = SORTED_PIECES * 512
+            words = raws[j][:].rearrange("p i k -> p (i k)").bitcast(F32)
+            sw = srt.tile([P, n], F32, name="sorted%d" % j, tag="sorted")
+            nc.scalar.copy(
+                out=sw[:].rearrange("p (g u w) -> p g u w", u=2, w=P),
+                in_=words[:, 0:n].rearrange("p (g w u) -> p g u w", w=P, u=2),
+            )
+            sorted_words[j] = sw
+
         def tjob(j):
             key = tjobs[j][0]
             words = raws[j][:].rearrange("p i k -> p (i k)").bitcast(F32)
@@ -97,19 +112,18 @@ def tile_paligemma2withexpertmodel_pa_kernel(
             for b in range(4):
                 tp = tpp.tile([P, 2, 256], F32, name="tp%d_%d" % (j, b), tag="tp")
                 for il in range(2):
-                    off = (2 * (b % 2) + il) * 512 + (b // 2) * 256
+                    piece = 2 * (b % 2) + il
+                    off = piece * 512 + (b // 2) * 256
                     for u in range(2):
-                        nc.tensor.transpose(
-                            tp[:, u, il * P : (il + 1) * P],
-                            words[:, off + u : off + 256 : 2],
-                            ident[:],
-                        )
+                        if j in sorted_words and piece < SORTED_PIECES:
+                            src = sorted_words[j][:, off + u * P : off + (u + 1) * P]
+                        else:
+                            src = words[:, off + u : off + 256 : 2]
+                        nc.tensor.transpose(tp[:, u, il * P : (il + 1) * P], src, ident[:])
                 nc.scalar.copy(
                     out=grouped[:, 256 * b : 256 * (b + 1), :].bitcast(F32),
                     in_=tp[:].rearrange("p u c -> p c u"),
                 )
-                if j < HEAD_JOBS and b % 2 == 1:
-                    warm(2, "scrap%d_%d" % (j, b))
             if key[0] == "x":
                 cd = xcp.tile([P, 1024], U32, name="xc%d" % j, tag="xc%d" % j, align_bytes=64)
                 sc = xcp.tile([P, 1024], U8, name="xs%d" % j, tag="xs%d" % j, align_bytes=64)
@@ -153,9 +167,13 @@ def tile_paligemma2withexpertmodel_pa_kernel(
             nc.vector.tensor_tensor(out=t_c[:, 1], in0=accs[1], in1=cb, op=MULT)
             nc.vector.tensor_tensor(out=t_s[:, 0], in0=accs[1], in1=sb, op=MULT)
             o = outp.tile([P, 4, 2, P], F32, name="o%d" % n, tag="o")
-            adder = nc.vector if n == len(units) - 1 else nc.gpsimd
-            adder.tensor_tensor(out=o[:, :, 0, :], in0=t_c[:, 0], in1=t_s[:, 0], op=SUB)
-            adder.tensor_tensor(out=o[:, :, 1, :], in0=t_c[:, 1], in1=t_s[:, 1], op=ADD)
+            last = len(units) - 1
+            sub_eng = nc.vector if n == last else nc.gpsimd
+            if n >= last - 1:
+                nc.vector.tensor_tensor(out=o[:, :, 1, :], in0=t_c[:, 1], in1=t_s[:, 1], op=ADD)
+            sub_eng.tensor_tensor(out=o[:, :, 0, :], in0=t_c[:, 0], in1=t_s[:, 0], op=SUB)
+            if n < last - 1:
+                nc.gpsimd.tensor_tensor(out=o[:, :, 1, :], in0=t_c[:, 1], in1=t_s[:, 1], op=ADD)
             b = m // 2
             rows = slice(pt * P, (pt + 1) * P)
             if s < 2:
@@ -178,6 +196,7 @@ def tile_paligemma2withexpertmodel_pa_kernel(
         done = 0
         issued = 0
         for j in range(len(tjobs)):
+            sort_words(j + 2)
             tjob(j)
             if j + RAW_BUFS < len(tjobs):
                 load(j + RAW_BUFS)

@@ -10,7 +10,6 @@ U8 = mybir.dt.uint8
 E5X4 = mybir.dt.float8_e5m2_x4
 MULT = mybir.AluOpType.mult
 ADD = mybir.AluOpType.add
-SUB = mybir.AluOpType.subtract
 
 FLOPS = 2 * 512 * 3072 * (2048 + 1024)
 
@@ -73,8 +72,8 @@ def tile_paligemma2withexpertmodel_pa_kernel(
 
         ident = const.tile([P, P], F32, name="ident", tag="ident")
         make_identity(nc, ident[:])
-        cos_t = const.tile([P, 4, P], BF16, name="cos_t", tag="cos_t")
-        sin_t = const.tile([P, 4, P], BF16, name="sin_t", tag="sin_t")
+        tab_a = const.tile([P, 4, 2, P], BF16, name="tab_a", tag="tab_a")
+        tab_b = const.tile([P, 4, 2, P], BF16, name="tab_b", tag="tab_b")
 
         zeros = const.tile([P, 512], BF16, name="zeros", tag="zeros")
         nc.vector.memset(zeros[:], 0.0)
@@ -156,24 +155,21 @@ def tile_paligemma2withexpertmodel_pa_kernel(
                         start=(g == 0),
                         stop=(g == npass - 1),
                     )
-                accs.append(acc[:].rearrange("p (h d) -> p h d", h=4))
+                accs.append(
+                    acc[:].rearrange("p (h d) -> p h d", h=4).unsqueeze(1).to_broadcast([P, 2, 4, P])
+                )
             pt = (m % 2) + (0 if st == "p" else 2)
-            cb = cos_t[:, pt, :].unsqueeze(1).to_broadcast([P, 4, P])
-            sb = sin_t[:, pt, :].unsqueeze(1).to_broadcast([P, 4, P])
-            t_c = ropep.tile([P, 2, 4, P], F32, name="t_c%d" % n, tag="t_c")
-            t_s = ropep.tile([P, 2, 4, P], F32, name="t_s%d" % n, tag="t_s")
-            nc.vector.tensor_tensor(out=t_c[:, 0], in0=accs[0], in1=cb, op=MULT)
-            nc.vector.tensor_tensor(out=t_s[:, 1], in0=accs[0], in1=sb, op=MULT)
-            nc.vector.tensor_tensor(out=t_c[:, 1], in0=accs[1], in1=cb, op=MULT)
-            nc.vector.tensor_tensor(out=t_s[:, 0], in0=accs[1], in1=sb, op=MULT)
+            t_a = ropep.tile([P, 2, 4, P], F32, name="t_a%d" % n, tag="t_a")
+            t_b = ropep.tile([P, 2, 4, P], F32, name="t_b%d" % n, tag="t_b")
+            nc.vector.tensor_tensor(
+                out=t_a[:], in0=accs[0], in1=tab_a[:, pt].unsqueeze(2).to_broadcast([P, 2, 4, P]), op=MULT
+            )
+            nc.vector.tensor_tensor(
+                out=t_b[:], in0=accs[1], in1=tab_b[:, pt].unsqueeze(2).to_broadcast([P, 2, 4, P]), op=MULT
+            )
             o = outp.tile([P, 4, 2, P], F32, name="o%d" % n, tag="o")
-            last = len(units) - 1
-            sub_eng = nc.vector if n == last else nc.gpsimd
-            if n >= last - 1:
-                nc.vector.tensor_tensor(out=o[:, :, 1, :], in0=t_c[:, 1], in1=t_s[:, 1], op=ADD)
-            sub_eng.tensor_tensor(out=o[:, :, 0, :], in0=t_c[:, 0], in1=t_s[:, 0], op=SUB)
-            if n < last - 1:
-                nc.gpsimd.tensor_tensor(out=o[:, :, 1, :], in0=t_c[:, 1], in1=t_s[:, 1], op=ADD)
+            adder = nc.vector if n == len(units) - 1 else nc.gpsimd
+            adder.tensor_tensor(out=o[:].rearrange("p h f d -> p f h d"), in0=t_a[:], in1=t_b[:], op=ADD)
             b = m // 2
             rows = slice(pt * P, (pt + 1) * P)
             if s < 2:
@@ -185,11 +181,11 @@ def tile_paligemma2withexpertmodel_pa_kernel(
                 in_=o[:].rearrange("p h f d -> p (h f d)"),
             )
 
-        for n in range(5):
+        for n in range(3):
             load(n)
-        nc.sync.dma_start(out=cos_t[:], in_=cos[0, :, 0, :].rearrange("(t p) d -> p t d", p=P))
-        nc.sync.dma_start(out=sin_t[:], in_=sin[0, :, 0, :].rearrange("(t p) d -> p t d", p=P))
-        for n in range(5, RAW_BUFS):
+        nc.sync.dma_start(out=tab_a[:, :, 0, :], in_=cos[0, :, 0, :].rearrange("(t p) d -> p t d", p=P))
+        nc.sync.dma_start(out=tab_a[:, :, 1, :], in_=sin[0, :, 0, :].rearrange("(t p) d -> p t d", p=P))
+        for n in range(3, RAW_BUFS):
             load(n)
         warm(WARM_FIRST, "scrap_first")
 
@@ -200,9 +196,12 @@ def tile_paligemma2withexpertmodel_pa_kernel(
             tjob(j)
             if j + RAW_BUFS < len(tjobs):
                 load(j + RAW_BUFS)
-            if j < 3:
+            if j < 2:
                 continue
-            quota = 4 * (j - 2) if j <= 10 else 32 + 8 * (j - 10)
+            if j == 2:
+                nc.vector.tensor_scalar_mul(out=tab_b[:, :, 0, :], in0=tab_a[:, :, 1, :], scalar1=-1.0)
+                nc.vector.tensor_copy(out=tab_b[:, :, 1, :], in_=tab_a[:, :, 0, :])
+            quota = min(4 * (j - 1), 32) if j <= 10 else 32 + 8 * (j - 10)
             if j == len(tjobs) - 1:
                 quota = 144
             while done < len(units) and issued < quota:

@@ -14,9 +14,11 @@ ADD = mybir.AluOpType.add
 FLOPS = 2 * 512 * 3072 * (2048 + 1024)
 
 P = 128
-RAW_BUFS = 10
-WARM_FIRST = 10
-FIRST_SORTED_JOB = 11
+RAW_BUFS = 7
+HEAD_JOBS = 4
+WARM_FIRST = 8
+WARM_JOBS = 3
+FIRST_SORTED_JOB = 14
 SORTED_PIECES = 3
 
 
@@ -28,38 +30,46 @@ def tile_paligemma2withexpertmodel_pa_kernel(
     wsrc = {"p": (wq0, wk0), "e": (wq1, wk1)}
     halves = {"p": 2, "e": 1}
 
-    def x_view(st, kh):
-        return xsrc[st][:, kh * 1024 : (kh + 1) * 1024].rearrange("(m p) k -> p m k", p=P)
+    def w_rows(st, s):
+        return (wsrc[st][0] if s < 2 else wsrc[st][1]), 1024 * (s % 2)
 
-    def w_view(st, s, f, kh):
-        w = wsrc[st][0] if s < 2 else wsrc[st][1]
-        r0 = 1024 * (s % 2)
-        v = w[r0 : r0 + 1024, kh * 1024 : (kh + 1) * 1024]
-        return v.rearrange("(h f p) k -> f p h k", f=2, p=P)[f]
+    def job_x(st, kh, m0, nt):
+        src = xsrc[st][m0 * P : (m0 + nt) * P, kh * 1024 : (kh + 1) * 1024]
+        return {"key": ("x", st, kh, m0), "kind": "x", "nt": nt, "place": list(range(nt)), "src": src}
 
-    def x_jobs(st):
-        return [(("x", st, kh), x_view(st, kh)) for kh in range(halves[st])]
+    def job_a(st, s, f, kh):
+        w, r0 = w_rows(st, s)
+        src = w[r0 : r0 + 1024, kh * 1024 : (kh + 1) * 1024]
+        view = src.rearrange("(h f p) k -> f p h k", f=2, p=P)[f]
+        return {"key": ("a", st, s, f, kh), "kind": "w", "nt": 4, "place": [0, 1, 2, 3], "view": view}
 
-    def w_jobs(st, s):
-        return [
-            (("w", st, s, f, kh), w_view(st, s, f, kh))
-            for f in range(2)
-            for kh in range(halves[st])
-        ]
+    def job_b(st, s, hh, kh):
+        w, r0 = w_rows(st, s)
+        src = w[r0 + 512 * hh : r0 + 512 * (hh + 1), kh * 1024 : (kh + 1) * 1024]
+        return {"key": ("b", st, s, hh, kh), "kind": "w", "nt": 4, "place": [0, 2, 1, 3], "src": src}
+
+    def jobs_a(st, s):
+        return [job_a(st, s, f, kh) for f in range(2) for kh in range(halves[st])]
+
+    def jobs_b(st, s):
+        return [job_b(st, s, hh, kh) for hh in range(2) for kh in range(halves[st])]
 
     tjobs = (
-        x_jobs("e") + w_jobs("e", 0) + w_jobs("e", 1) + x_jobs("p") + w_jobs("p", 0)
-        + w_jobs("e", 2) + w_jobs("p", 1) + w_jobs("p", 2)
+        [job_x("e", 0, 0, 2), job_b("e", 0, 0, 0), job_x("e", 0, 2, 2), job_b("e", 0, 1, 0)]
+        + jobs_a("e", 1) + jobs_a("e", 2)
+        + [job_x("p", 0, 0, 4), job_x("p", 1, 0, 4)]
+        + jobs_a("p", 0) + jobs_a("p", 1) + jobs_b("p", 2)
     )
-    units = [
-        (st, s, m)
-        for (st, s) in (("e", 0), ("e", 1), ("p", 0), ("e", 2), ("p", 1), ("p", 2))
-        for m in range(4)
-    ]
+    units = (
+        [("b", "e", 0, hh, m) for hh in range(2) for m in range(4)]
+        + [("a", st, s, 0, m) for (st, s) in (("e", 1), ("e", 2), ("p", 0), ("p", 1)) for m in range(4)]
+        + [("b", "p", 2, hh, m) for hh in range(2) for m in range(4)]
+    )
 
     with ExitStack() as ctx:
         ctx.enter_context(tc.manual_schedule())
         const = ctx.enter_context(tc.tile_pool(name="const", bufs=1))
+        piecep = ctx.enter_context(tc.tile_pool(name="piecep", bufs=1))
         rawp = ctx.enter_context(tc.tile_pool(name="rawp", bufs=RAW_BUFS))
         grp = ctx.enter_context(tc.tile_pool(name="grp", bufs=3))
         srt = ctx.enter_context(tc.tile_pool(name="srt", bufs=3))
@@ -78,54 +88,85 @@ def tile_paligemma2withexpertmodel_pa_kernel(
         zeros = const.tile([P, 512], BF16, name="zeros", tag="zeros")
         nc.vector.memset(zeros[:], 0.0)
 
-        raws = {}
+        words_of = {}
         sorted_words = {}
         codes = {}
+        bank_turn = [0]
 
         def warm(count, name):
             scrap = accp.tile([P, 512], F32, name=name, tag="acc0")
             for i in range(count):
                 nc.tensor.matmul(scrap[:], lhsT=zeros[:, 0:P], rhs=zeros[:], start=True, stop=True)
 
+        def piece_order(job):
+            return sorted(range(job["nt"]), key=lambda i: job["place"][i])
+
         def load(n):
+            job = tjobs[n]
+            nt = job["nt"]
+            if n < HEAD_JOBS:
+                for i in piece_order(job):
+                    pc = piecep.tile([P, 1024], BF16, name="pc%d_%d" % (n, i), tag="pc%d_%d" % (n, i))
+                    nc.sync.dma_start(out=pc[:], in_=job["src"][i * P : (i + 1) * P, :])
+                    words_of[(n, i)] = pc[:].bitcast(F32)
+                return
             raw = rawp.tile([P, 4, 1024], BF16, name="raw%d" % n, tag="raw")
-            nc.sync.dma_start(out=raw[:], in_=tjobs[n][1])
-            raws[n] = raw
+            view = job["view"] if "view" in job else job["src"].rearrange("(i p) k -> p i k", p=P)
+            nc.sync.dma_start(out=raw[:], in_=view)
+            words = raw[:].rearrange("p i k -> p (i k)").bitcast(F32)
+            for i in range(nt):
+                words_of[(n, i)] = words[:, i * 512 : (i + 1) * 512]
+            words_of[n] = words
 
         def sort_words(j):
             if j < FIRST_SORTED_JOB or j >= len(tjobs):
                 return
             n = SORTED_PIECES * 512
-            words = raws[j][:].rearrange("p i k -> p (i k)").bitcast(F32)
             sw = srt.tile([P, n], F32, name="sorted%d" % j, tag="sorted")
             nc.scalar.copy(
                 out=sw[:].rearrange("p (g u w) -> p g u w", u=2, w=P),
-                in_=words[:, 0:n].rearrange("p (g w u) -> p g u w", w=P, u=2),
+                in_=words_of[j][:, 0:n].rearrange("p (g w u) -> p g u w", w=P, u=2),
             )
             sorted_words[j] = sw
 
         def tjob(j):
-            key = tjobs[j][0]
-            words = raws[j][:].rearrange("p i k -> p (i k)").bitcast(F32)
-            grouped = grp.tile([P, 1024, 4], BF16, name="grouped%d" % j, tag="grouped", align_bytes=64)
-            for b in range(4):
-                tp = tpp.tile([P, 2, 256], F32, name="tp%d_%d" % (j, b), tag="tp")
-                for il in range(2):
-                    piece = 2 * (b % 2) + il
-                    off = piece * 512 + (b // 2) * 256
-                    for u in range(2):
-                        if j in sorted_words and piece < SORTED_PIECES:
-                            src = sorted_words[j][:, off + u * P : off + (u + 1) * P]
-                        else:
-                            src = words[:, off + u : off + 256 : 2]
-                        nc.tensor.transpose(tp[:, u, il * P : (il + 1) * P], src, ident[:])
-                nc.scalar.copy(
-                    out=grouped[:, 256 * b : 256 * (b + 1), :].bitcast(F32),
-                    in_=tp[:].rearrange("p u c -> p c u"),
-                )
-            if key[0] == "x":
-                cd = xcp.tile([P, 1024], U32, name="xc%d" % j, tag="xc%d" % j, align_bytes=64)
-                sc = xcp.tile([P, 1024], U8, name="xs%d" % j, tag="xs%d" % j, align_bytes=64)
+            job = tjobs[j]
+            nt = job["nt"]
+            place = job["place"]
+            grouped = grp.tile([P, 256 * nt, 4], BF16, name="grouped%d" % j, tag="grouped", align_bytes=64)
+            if j < HEAD_JOBS:
+                order = [(i, g) for i in piece_order(job) for g in range(2)]
+            else:
+                order = [(place.index(cb % nt), cb // nt) for cb in range(2 * nt)]
+            banks = {}
+            filled = {}
+            done_t = 0
+            for (i, g) in order:
+                cb = g * nt + place[i]
+                b = cb // 2
+                il = cb % 2
+                if b not in banks:
+                    banks[b] = tpp.tile([P, 2, 256], F32, name="tp%d_%d" % (j, b), tag="tp")
+                    filled[b] = 0
+                for u in range(2):
+                    if j in sorted_words and i < SORTED_PIECES:
+                        off = i * 512 + g * 256
+                        src = sorted_words[j][:, off + u * P : off + (u + 1) * P]
+                    else:
+                        src = words_of[(j, i)][:, g * 256 + u : (g + 1) * 256 : 2]
+                    nc.tensor.transpose(banks[b][:, u, il * P : (il + 1) * P], src, ident[:])
+                done_t += 2
+                filled[b] += 1
+                if filled[b] == 2:
+                    nc.scalar.copy(
+                        out=grouped[:, 256 * b : 256 * (b + 1), :].bitcast(F32),
+                        in_=banks[b][:].rearrange("p u c -> p c u"),
+                    )
+                if j < WARM_JOBS and done_t % 8 == 0:
+                    warm(2, "scrap%d_%d" % (j, done_t))
+            if job["kind"] == "x":
+                cd = xcp.tile([P, 256 * nt], U32, name="xc%d" % j, tag="xc%d" % j, align_bytes=64)
+                sc = xcp.tile([P, 256 * nt], U8, name="xs%d" % j, tag="xs%d" % j, align_bytes=64)
             else:
                 cd = wcp.tile([P, 1024], U32, name="wc%d" % j, tag="wc", align_bytes=64)
                 sc = wcp.tile([P, 1024], U8, name="ws%d" % j, tag="ws", align_bytes=64)
@@ -134,58 +175,86 @@ def tile_paligemma2withexpertmodel_pa_kernel(
                 scales=sc[:],
                 in_=grouped[:].rearrange("p c t -> p (c t)"),
             )
-            codes[key] = (cd, sc)
+            codes[job["key"]] = (cd, sc)
+
+        def x_operand(st, m, g):
+            if st == "e":
+                xc, xs = codes[("x", "e", 0, 2 * (m // 2))]
+                c0 = g * 256 + (m % 2) * P
+            else:
+                xc, xs = codes[("x", "p", g // 2, 0)]
+                c0 = (g % 2) * 512 + m * P
+            return xc[:, c0 : c0 + P].bitcast(E5X4), xs[:, c0 : c0 + P]
+
+        def mx_group(acc, st, m, wkey):
+            npass = 2 * halves[st]
+            for g in range(npass):
+                lhs, lhs_scale = x_operand(st, m, g)
+                wc, ws = codes[wkey + (g // 2,)]
+                c0 = (g % 2) * 512
+                nc.tensor.matmul_mx(
+                    out=acc[:],
+                    lhsT=lhs,
+                    lhsT_scale=lhs_scale,
+                    rhs=wc[:, c0 : c0 + 512].bitcast(E5X4),
+                    rhs_scale=ws[:, c0 : c0 + 512],
+                    start=(g == 0),
+                    stop=(g == npass - 1),
+                )
 
         def unit(n):
-            st, s, m = units[n]
-            npass = 2 * halves[st]
-            accs = []
-            for f in range(2):
-                acc = accp.tile([P, 512], F32, name="acc%d_%d" % (n, f), tag="acc%d" % f)
-                for g in range(npass):
-                    xc, xs = codes[("x", st, g // 2)]
-                    wc, ws = codes[("w", st, s, f, g // 2)]
-                    c0 = (g % 2) * 512
-                    nc.tensor.matmul_mx(
-                        out=acc[:],
-                        lhsT=xc[:, c0 + m * P : c0 + (m + 1) * P].bitcast(E5X4),
-                        lhsT_scale=xs[:, c0 + m * P : c0 + (m + 1) * P],
-                        rhs=wc[:, c0 : c0 + 512].bitcast(E5X4),
-                        rhs_scale=ws[:, c0 : c0 + 512],
-                        start=(g == 0),
-                        stop=(g == npass - 1),
-                    )
-                accs.append(
-                    acc[:].rearrange("p (h d) -> p h d", h=4).unsqueeze(1).to_broadcast([P, 2, 4, P])
-                )
+            form, st, s, hh, m = units[n]
+            if form == "a":
+                nh = 4
+                h0 = 0
+                acc0 = accp.tile([P, 512], F32, name="acc%d_0" % n, tag="acc0")
+                mx_group(acc0, st, m, ("a", st, s, 0))
+                acc1 = accp.tile([P, 512], F32, name="acc%d_1" % n, tag="acc1")
+                mx_group(acc1, st, m, ("a", st, s, 1))
+                x1 = acc0[:]
+                x2 = acc1[:]
+            else:
+                nh = 2
+                h0 = 2 * hh
+                acc = accp.tile([P, 512], F32, name="acc%d" % n, tag="acc%d" % (bank_turn[0] % 2))
+                bank_turn[0] += 1
+                mx_group(acc, st, m, ("b", st, s, hh))
+                x1 = acc[:, 0:256]
+                x2 = acc[:, 256:512]
+            shape = [P, 2, nh, P]
+            x1 = x1.rearrange("p (h d) -> p h d", h=nh).unsqueeze(1).to_broadcast(shape)
+            x2 = x2.rearrange("p (h d) -> p h d", h=nh).unsqueeze(1).to_broadcast(shape)
             pt = (m % 2) + (0 if st == "p" else 2)
-            t_a = ropep.tile([P, 2, 4, P], F32, name="t_a%d" % n, tag="t_a")
-            t_b = ropep.tile([P, 2, 4, P], F32, name="t_b%d" % n, tag="t_b")
+            t_a = ropep.tile(shape, F32, name="t_a%d" % n, tag="t_a")
+            t_b = ropep.tile(shape, F32, name="t_b%d" % n, tag="t_b")
             nc.vector.tensor_tensor(
-                out=t_a[:], in0=accs[0], in1=tab_a[:, pt].unsqueeze(2).to_broadcast([P, 2, 4, P]), op=MULT
+                out=t_a[:], in0=x1, in1=tab_a[:, pt].unsqueeze(2).to_broadcast(shape), op=MULT
             )
             nc.vector.tensor_tensor(
-                out=t_b[:], in0=accs[1], in1=tab_b[:, pt].unsqueeze(2).to_broadcast([P, 2, 4, P]), op=MULT
+                out=t_b[:], in0=x2, in1=tab_b[:, pt].unsqueeze(2).to_broadcast(shape), op=MULT
             )
-            o = outp.tile([P, 4, 2, P], F32, name="o%d" % n, tag="o")
+            o = outp.tile([P, nh, 2, P], F32, name="o%d" % n, tag="o")
             adder = nc.vector if n == len(units) - 1 else nc.gpsimd
             adder.tensor_tensor(out=o[:].rearrange("p h f d -> p f h d"), in0=t_a[:], in1=t_b[:], op=ADD)
             b = m // 2
             rows = slice(pt * P, (pt + 1) * P)
             if s < 2:
-                dst = out_0[b, rows, 4 * s : 4 * s + 4, :]
+                dst = out_0[b, rows, 4 * s + h0 : 4 * s + h0 + nh, :]
             else:
-                dst = out_1[b, rows, :, :]
+                dst = out_1[b, rows, h0 : h0 + nh, :]
             nc.sync.dma_start(
                 out=dst.rearrange("p h d -> p (h d)"),
                 in_=o[:].rearrange("p h f d -> p (h f d)"),
             )
 
-        for n in range(3):
-            load(n)
+        def passes_of(n):
+            return (4 if units[n][0] == "a" else 2) * halves[units[n][1]]
+
+        load(0)
+        load(1)
         nc.sync.dma_start(out=tab_a[:, :, 0, :], in_=cos[0, :, 0, :].rearrange("(t p) d -> p t d", p=P))
         nc.sync.dma_start(out=tab_a[:, :, 1, :], in_=sin[0, :, 0, :].rearrange("(t p) d -> p t d", p=P))
-        for n in range(3, RAW_BUFS):
+        for n in range(2, HEAD_JOBS + RAW_BUFS):
             load(n)
         warm(WARM_FIRST, "scrap_first")
 
@@ -194,17 +263,17 @@ def tile_paligemma2withexpertmodel_pa_kernel(
         for j in range(len(tjobs)):
             sort_words(j + 2)
             tjob(j)
-            if j + RAW_BUFS < len(tjobs):
+            if j >= HEAD_JOBS and j + RAW_BUFS < len(tjobs):
                 load(j + RAW_BUFS)
             if j < 2:
                 continue
             if j == 2:
                 nc.vector.tensor_scalar_mul(out=tab_b[:, :, 0, :], in0=tab_a[:, :, 1, :], scalar1=-1.0)
                 nc.vector.tensor_copy(out=tab_b[:, :, 1, :], in_=tab_a[:, :, 0, :])
-            quota = min(4 * (j - 1), 32) if j <= 10 else 32 + 8 * (j - 10)
+            quota = 4 * (j - 1) if j <= 13 else 48 + 8 * (j - 13)
             if j == len(tjobs) - 1:
                 quota = 144
             while done < len(units) and issued < quota:
-                issued += 4 * halves[units[done][0]]
+                issued += passes_of(done)
                 unit(done)
                 done += 1

@@ -15,10 +15,10 @@ FLOPS = 2 * 512 * 3072 * (2048 + 1024)
 
 P = 128
 RAW_BUFS = 7
-HEAD_JOBS = 4
+HEAD_JOBS = 6
 WARM_FIRST = 8
-WARM_JOBS = 3
-FIRST_SORTED_JOB = 14
+WARM_TRANSPOSES = 24
+FIRST_SORTED_JOB = 16
 SORTED_PIECES = 3
 
 
@@ -55,7 +55,8 @@ def tile_paligemma2withexpertmodel_pa_kernel(
         return [job_b(st, s, hh, kh) for hh in range(2) for kh in range(halves[st])]
 
     tjobs = (
-        [job_x("e", 0, 0, 2), job_b("e", 0, 0, 0), job_x("e", 0, 2, 2), job_b("e", 0, 1, 0)]
+        [job_x("e", 0, 0, 1), job_b("e", 0, 0, 0), job_x("e", 0, 1, 1), job_x("e", 0, 2, 1), job_x("e", 0, 3, 1)]
+        + [job_b("e", 0, 1, 0)]
         + jobs_a("e", 1) + jobs_a("e", 2)
         + [job_x("p", 0, 0, 4), job_x("p", 1, 0, 4)]
         + jobs_a("p", 0) + jobs_a("p", 1) + jobs_b("p", 2)
@@ -91,7 +92,10 @@ def tile_paligemma2withexpertmodel_pa_kernel(
         words_of = {}
         sorted_words = {}
         codes = {}
+        state = {}
+        accs = {}
         bank_turn = [0]
+        head_t = [0]
 
         def warm(count, name):
             scrap = accp.tile([P, 512], F32, name=name, tag="acc0")
@@ -129,19 +133,36 @@ def tile_paligemma2withexpertmodel_pa_kernel(
             )
             sorted_words[j] = sw
 
-        def tjob(j):
+        def quantise(j, c0, c1):
+            grouped, cd, sc = state[j]["tiles"]
+            nc.vector.quantize_mx(
+                out=cd[:, c0:c1].bitcast(E5X4),
+                scales=sc[:, c0:c1],
+                in_=grouped[:, c0:c1, :].rearrange("p c t -> p (c t)"),
+            )
+
+        def transposes(j, first, count):
             job = tjobs[j]
             nt = job["nt"]
             place = job["place"]
-            grouped = grp.tile([P, 256 * nt, 4], BF16, name="grouped%d" % j, tag="grouped", align_bytes=64)
+            if j not in state:
+                grouped = grp.tile([P, 256 * nt, 4], BF16, name="grouped%d" % j, tag="grouped", align_bytes=64)
+                if job["kind"] == "x":
+                    cd = xcp.tile([P, 256 * nt], U32, name="xc%d" % j, tag="xc%d" % j, align_bytes=64)
+                    sc = xcp.tile([P, 256 * nt], U8, name="xs%d" % j, tag="xs%d" % j, align_bytes=64)
+                else:
+                    cd = wcp.tile([P, 1024], U32, name="wc%d" % j, tag="wc", align_bytes=64)
+                    sc = wcp.tile([P, 1024], U8, name="ws%d" % j, tag="ws", align_bytes=64)
+                state[j] = {"tiles": (grouped, cd, sc), "banks": {}, "filled": {}}
+                codes[job["key"]] = (cd, sc)
+            grouped = state[j]["tiles"][0]
+            banks = state[j]["banks"]
+            filled = state[j]["filled"]
             if j < HEAD_JOBS:
                 order = [(i, g) for i in piece_order(job) for g in range(2)]
             else:
                 order = [(place.index(cb % nt), cb // nt) for cb in range(2 * nt)]
-            banks = {}
-            filled = {}
-            done_t = 0
-            for (i, g) in order:
+            for (i, g) in order[first : first + count]:
                 cb = g * nt + place[i]
                 b = cb // 2
                 il = cb % 2
@@ -155,32 +176,29 @@ def tile_paligemma2withexpertmodel_pa_kernel(
                     else:
                         src = words_of[(j, i)][:, g * 256 + u : (g + 1) * 256 : 2]
                     nc.tensor.transpose(banks[b][:, u, il * P : (il + 1) * P], src, ident[:])
-                done_t += 2
                 filled[b] += 1
                 if filled[b] == 2:
                     nc.scalar.copy(
                         out=grouped[:, 256 * b : 256 * (b + 1), :].bitcast(F32),
                         in_=banks[b][:].rearrange("p u c -> p c u"),
                     )
-                if j < WARM_JOBS and done_t % 8 == 0:
-                    warm(2, "scrap%d_%d" % (j, done_t))
-            if job["kind"] == "x":
-                cd = xcp.tile([P, 256 * nt], U32, name="xc%d" % j, tag="xc%d" % j, align_bytes=64)
-                sc = xcp.tile([P, 256 * nt], U8, name="xs%d" % j, tag="xs%d" % j, align_bytes=64)
-            else:
-                cd = wcp.tile([P, 1024], U32, name="wc%d" % j, tag="wc", align_bytes=64)
-                sc = wcp.tile([P, 1024], U8, name="ws%d" % j, tag="ws", align_bytes=64)
-            nc.vector.quantize_mx(
-                out=cd[:].bitcast(E5X4),
-                scales=sc[:],
-                in_=grouped[:].rearrange("p c t -> p (c t)"),
-            )
-            codes[job["key"]] = (cd, sc)
+                    if j < HEAD_JOBS:
+                        quantise(j, 256 * b, 256 * (b + 1))
+                if head_t[0] < WARM_TRANSPOSES:
+                    head_t[0] += 2
+                    if head_t[0] % 8 == 0:
+                        warm(2, "scrap%d" % head_t[0])
+
+        def tjob(j):
+            nt = tjobs[j]["nt"]
+            transposes(j, 0, 2 * nt)
+            if j >= HEAD_JOBS:
+                quantise(j, 0, 256 * nt)
 
         def x_operand(st, m, g):
             if st == "e":
-                xc, xs = codes[("x", "e", 0, 2 * (m // 2))]
-                c0 = g * 256 + (m % 2) * P
+                xc, xs = codes[("x", "e", 0, m)]
+                c0 = g * P
             else:
                 xc, xs = codes[("x", "p", g // 2, 0)]
                 c0 = (g % 2) * 512 + m * P
@@ -202,25 +220,25 @@ def tile_paligemma2withexpertmodel_pa_kernel(
                     stop=(g == npass - 1),
                 )
 
-        def unit(n):
+        def unit_mx(n):
             form, st, s, hh, m = units[n]
             if form == "a":
-                nh = 4
-                h0 = 0
                 acc0 = accp.tile([P, 512], F32, name="acc%d_0" % n, tag="acc0")
                 mx_group(acc0, st, m, ("a", st, s, 0))
                 acc1 = accp.tile([P, 512], F32, name="acc%d_1" % n, tag="acc1")
                 mx_group(acc1, st, m, ("a", st, s, 1))
-                x1 = acc0[:]
-                x2 = acc1[:]
+                accs[n] = (acc0[:], acc1[:])
             else:
-                nh = 2
-                h0 = 2 * hh
                 acc = accp.tile([P, 512], F32, name="acc%d" % n, tag="acc%d" % (bank_turn[0] % 2))
                 bank_turn[0] += 1
                 mx_group(acc, st, m, ("b", st, s, hh))
-                x1 = acc[:, 0:256]
-                x2 = acc[:, 256:512]
+                accs[n] = (acc[:, 0:256], acc[:, 256:512])
+
+        def unit_rope(n):
+            form, st, s, hh, m = units[n]
+            nh = 4 if form == "a" else 2
+            h0 = 0 if form == "a" else 2 * hh
+            x1, x2 = accs[n]
             shape = [P, 2, nh, P]
             x1 = x1.rearrange("p (h d) -> p h d", h=nh).unsqueeze(1).to_broadcast(shape)
             x2 = x2.rearrange("p (h d) -> p h d", h=nh).unsqueeze(1).to_broadcast(shape)
@@ -252,28 +270,43 @@ def tile_paligemma2withexpertmodel_pa_kernel(
 
         load(0)
         load(1)
+        load(2)
         nc.sync.dma_start(out=tab_a[:, :, 0, :], in_=cos[0, :, 0, :].rearrange("(t p) d -> p t d", p=P))
         nc.sync.dma_start(out=tab_a[:, :, 1, :], in_=sin[0, :, 0, :].rearrange("(t p) d -> p t d", p=P))
-        for n in range(2, HEAD_JOBS + RAW_BUFS):
+        for n in range(3, HEAD_JOBS + RAW_BUFS):
             load(n)
         warm(WARM_FIRST, "scrap_first")
 
-        done = 0
-        issued = 0
-        for j in range(len(tjobs)):
+        tjob(0)
+        tjob(1)
+        tjob(2)
+        nc.vector.tensor_scalar_mul(out=tab_b[:, :, 0, :], in0=tab_a[:, :, 1, :], scalar1=-1.0)
+        nc.vector.tensor_copy(out=tab_b[:, :, 1, :], in_=tab_a[:, :, 0, :])
+        tjob(3)
+        unit_mx(0)
+        unit_mx(1)
+        unit_rope(0)
+        tjob(4)
+        unit_rope(1)
+        transposes(5, 0, 4)
+        unit_mx(2)
+        unit_mx(3)
+        unit_rope(2)
+        transposes(5, 4, 4)
+        unit_rope(3)
+
+        done = 4
+        issued = 8
+        for j in range(HEAD_JOBS, len(tjobs)):
             sort_words(j + 2)
             tjob(j)
-            if j >= HEAD_JOBS and j + RAW_BUFS < len(tjobs):
+            if j + RAW_BUFS < len(tjobs):
                 load(j + RAW_BUFS)
-            if j < 2:
-                continue
-            if j == 2:
-                nc.vector.tensor_scalar_mul(out=tab_b[:, :, 0, :], in0=tab_a[:, :, 1, :], scalar1=-1.0)
-                nc.vector.tensor_copy(out=tab_b[:, :, 1, :], in_=tab_a[:, :, 0, :])
-            quota = 4 * (j - 1) if j <= 13 else 48 + 8 * (j - 13)
+            quota = 4 * (j - 3) if j <= 15 else 48 + 8 * (j - 15)
             if j == len(tjobs) - 1:
                 quota = 144
             while done < len(units) and issued < quota:
                 issued += passes_of(done)
-                unit(done)
+                unit_mx(done)
+                unit_rope(done)
                 done += 1

@@ -20,6 +20,12 @@ WARM_FIRST = 8
 WARM_TRANSPOSES = 24
 FIRST_SORTED_JOB = 16
 SORTED_PIECES = 3
+SORT_AHEAD = 1
+STORE_LAG = 0
+OUT_BUFS = 6
+ROPE_BUFS = 3
+ADD_SPLIT = 1
+T_AHEAD = 1
 
 
 def tile_paligemma2withexpertmodel_pa_kernel(
@@ -76,8 +82,8 @@ def tile_paligemma2withexpertmodel_pa_kernel(
         srt = ctx.enter_context(tc.tile_pool(name="srt", bufs=3))
         wcp = ctx.enter_context(tc.tile_pool(name="wcp", bufs=8))
         xcp = ctx.enter_context(tc.tile_pool(name="xcp", bufs=1))
-        ropep = ctx.enter_context(tc.tile_pool(name="ropep", bufs=3))
-        outp = ctx.enter_context(tc.tile_pool(name="outp", bufs=6))
+        ropep = ctx.enter_context(tc.tile_pool(name="ropep", bufs=ROPE_BUFS))
+        outp = ctx.enter_context(tc.tile_pool(name="outp", bufs=OUT_BUFS))
         tpp = ctx.enter_context(tc.psum_pool(name="tpp", bufs=4))
         accp = ctx.enter_context(tc.psum_pool(name="accp", bufs=2))
 
@@ -96,6 +102,8 @@ def tile_paligemma2withexpertmodel_pa_kernel(
         accs = {}
         bank_turn = [0]
         head_t = [0]
+        waiting = []
+        loads_left = [True]
 
         def warm(count, name):
             scrap = accp.tile([P, 512], F32, name=name, tag="acc0")
@@ -134,7 +142,18 @@ def tile_paligemma2withexpertmodel_pa_kernel(
             sorted_words[j] = sw
 
         def quantise(j, c0, c1):
-            grouped, cd, sc = state[j]["tiles"]
+            job = tjobs[j]
+            nt = job["nt"]
+            if job["key"] not in codes:
+                if job["kind"] == "x":
+                    cd = xcp.tile([P, 256 * nt], U32, name="xc%d" % j, tag="xc%d" % j, align_bytes=64)
+                    sc = xcp.tile([P, 256 * nt], U8, name="xs%d" % j, tag="xs%d" % j, align_bytes=64)
+                else:
+                    cd = wcp.tile([P, 1024], U32, name="wc%d" % j, tag="wc", align_bytes=64)
+                    sc = wcp.tile([P, 1024], U8, name="ws%d" % j, tag="ws", align_bytes=64)
+                codes[job["key"]] = (cd, sc)
+            grouped = state[j]["grouped"]
+            cd, sc = codes[job["key"]]
             nc.vector.quantize_mx(
                 out=cd[:, c0:c1].bitcast(E5X4),
                 scales=sc[:, c0:c1],
@@ -147,15 +166,8 @@ def tile_paligemma2withexpertmodel_pa_kernel(
             place = job["place"]
             if j not in state:
                 grouped = grp.tile([P, 256 * nt, 4], BF16, name="grouped%d" % j, tag="grouped", align_bytes=64)
-                if job["kind"] == "x":
-                    cd = xcp.tile([P, 256 * nt], U32, name="xc%d" % j, tag="xc%d" % j, align_bytes=64)
-                    sc = xcp.tile([P, 256 * nt], U8, name="xs%d" % j, tag="xs%d" % j, align_bytes=64)
-                else:
-                    cd = wcp.tile([P, 1024], U32, name="wc%d" % j, tag="wc", align_bytes=64)
-                    sc = wcp.tile([P, 1024], U8, name="ws%d" % j, tag="ws", align_bytes=64)
-                state[j] = {"tiles": (grouped, cd, sc), "banks": {}, "filled": {}}
-                codes[job["key"]] = (cd, sc)
-            grouped = state[j]["tiles"][0]
+                state[j] = {"grouped": grouped, "banks": {}, "filled": {}}
+            grouped = state[j]["grouped"]
             banks = state[j]["banks"]
             filled = state[j]["filled"]
             if j < HEAD_JOBS:
@@ -253,13 +265,27 @@ def tile_paligemma2withexpertmodel_pa_kernel(
             )
             o = outp.tile([P, nh, 2, P], F32, name="o%d" % n, tag="o")
             adder = nc.vector if n == len(units) - 1 else nc.gpsimd
-            adder.tensor_tensor(out=o[:].rearrange("p h f d -> p f h d"), in0=t_a[:], in1=t_b[:], op=ADD)
+            parts = ADD_SPLIT if (form == "a" and adder is nc.gpsimd) else 1
+            hp = nh // parts
+            for q in range(parts):
+                adder.tensor_tensor(
+                    out=o[:, q * hp : (q + 1) * hp].rearrange("p h f d -> p f h d"),
+                    in0=t_a[:, :, q * hp : (q + 1) * hp, :],
+                    in1=t_b[:, :, q * hp : (q + 1) * hp, :],
+                    op=ADD,
+                )
             b = m // 2
             rows = slice(pt * P, (pt + 1) * P)
             if s < 2:
                 dst = out_0[b, rows, 4 * s + h0 : 4 * s + h0 + nh, :]
             else:
                 dst = out_1[b, rows, h0 : h0 + nh, :]
+            waiting.append((dst, o))
+            while len(waiting) > (STORE_LAG if loads_left[0] else 0):
+                store()
+
+        def store():
+            dst, o = waiting.pop(0)
             nc.sync.dma_start(
                 out=dst.rearrange("p h d -> p (h d)"),
                 in_=o[:].rearrange("p h f d -> p (h f d)"),
@@ -297,11 +323,19 @@ def tile_paligemma2withexpertmodel_pa_kernel(
 
         done = 4
         issued = 8
+        for jt in range(HEAD_JOBS, HEAD_JOBS + T_AHEAD):
+            transposes(jt, 0, 8)
+            load(jt + RAW_BUFS)
         for j in range(HEAD_JOBS, len(tjobs)):
-            sort_words(j + 2)
-            tjob(j)
-            if j + RAW_BUFS < len(tjobs):
-                load(j + RAW_BUFS)
+            jt = j + T_AHEAD
+            sort_words(jt + SORT_AHEAD)
+            if jt < len(tjobs):
+                transposes(jt, 0, 8)
+            quantise(j, 0, 1024)
+            if jt + RAW_BUFS < len(tjobs):
+                load(jt + RAW_BUFS)
+            if jt + RAW_BUFS >= len(tjobs) - 1:
+                loads_left[0] = False
             quota = 4 * (j - 3) if j <= 15 else 48 + 8 * (j - 15)
             if j == len(tjobs) - 1:
                 quota = 144

@@ -26,6 +26,10 @@ OUT_BUFS = 6
 ROPE_BUFS = 3
 ADD_SPLIT = 1
 T_AHEAD = 1
+ASSIST = ()
+MERGE_B = False
+LAST_A = True
+HEAD_Q_BANKS = True
 
 
 def tile_paligemma2withexpertmodel_pa_kernel(
@@ -65,12 +69,12 @@ def tile_paligemma2withexpertmodel_pa_kernel(
         + [job_b("e", 0, 1, 0)]
         + jobs_a("e", 1) + jobs_a("e", 2)
         + [job_x("p", 0, 0, 4), job_x("p", 1, 0, 4)]
-        + jobs_a("p", 0) + jobs_a("p", 1) + jobs_b("p", 2)
+        + jobs_a("p", 0) + jobs_a("p", 1) + (jobs_a("p", 2) if LAST_A else jobs_b("p", 2))
     )
     units = (
         [("b", "e", 0, hh, m) for hh in range(2) for m in range(4)]
         + [("a", st, s, 0, m) for (st, s) in (("e", 1), ("e", 2), ("p", 0), ("p", 1)) for m in range(4)]
-        + [("b", "p", 2, hh, m) for hh in range(2) for m in range(4)]
+        + ([("a", "p", 2, 0, m) for m in range(4)] if LAST_A else [("b", "p", 2, hh, m) for hh in range(2) for m in range(4)])
     )
 
     with ExitStack() as ctx:
@@ -84,6 +88,7 @@ def tile_paligemma2withexpertmodel_pa_kernel(
         xcp = ctx.enter_context(tc.tile_pool(name="xcp", bufs=1))
         ropep = ctx.enter_context(tc.tile_pool(name="ropep", bufs=ROPE_BUFS))
         outp = ctx.enter_context(tc.tile_pool(name="outp", bufs=OUT_BUFS))
+        asp = ctx.enter_context(tc.tile_pool(name="asp", bufs=2))
         tpp = ctx.enter_context(tc.psum_pool(name="tpp", bufs=4))
         accp = ctx.enter_context(tc.psum_pool(name="accp", bufs=2))
 
@@ -194,8 +199,10 @@ def tile_paligemma2withexpertmodel_pa_kernel(
                         out=grouped[:, 256 * b : 256 * (b + 1), :].bitcast(F32),
                         in_=banks[b][:].rearrange("p u c -> p c u"),
                     )
-                    if j < HEAD_JOBS:
+                    if j < HEAD_JOBS and (HEAD_Q_BANKS or nt == 1):
                         quantise(j, 256 * b, 256 * (b + 1))
+                    elif j < HEAD_JOBS and len(filled) == nt and min(filled.values()) == 2:
+                        quantise(j, 0, 256 * nt)
                 if head_t[0] < WARM_TRANSPOSES:
                     head_t[0] += 2
                     if head_t[0] % 8 == 0:
@@ -260,9 +267,16 @@ def tile_paligemma2withexpertmodel_pa_kernel(
             nc.vector.tensor_tensor(
                 out=t_a[:], in0=x1, in1=tab_a[:, pt].unsqueeze(2).to_broadcast(shape), op=MULT
             )
-            nc.vector.tensor_tensor(
-                out=t_b[:], in0=x2, in1=tab_b[:, pt].unsqueeze(2).to_broadcast(shape), op=MULT
-            )
+            if n in ASSIST:
+                xs = asp.tile([P, nh, P], F32, name="xs%d" % n, tag="xs")
+                nc.scalar.copy(out=xs[:], in_=accs[n][1].rearrange("p (h d) -> p h d", h=nh))
+                nc.gpsimd.tensor_tensor(
+                    out=t_b[:], in0=xs[:].unsqueeze(1).to_broadcast(shape), in1=tab_b[:, pt].unsqueeze(2).to_broadcast(shape), op=MULT
+                )
+            else:
+                nc.vector.tensor_tensor(
+                    out=t_b[:], in0=x2, in1=tab_b[:, pt].unsqueeze(2).to_broadcast(shape), op=MULT
+                )
             o = outp.tile([P, nh, 2, P], F32, name="o%d" % n, tag="o")
             adder = nc.vector if n == len(units) - 1 else nc.gpsimd
             parts = ADD_SPLIT if (form == "a" and adder is nc.gpsimd) else 1

@@ -18,7 +18,7 @@ RAW_BUFS = 7
 HEAD_JOBS = 6
 WARM_FIRST = 8
 WARM_TRANSPOSES = 24
-FIRST_SORTED_JOB = 16
+FIRST_SORTED_JOB = 18
 SORTED_PIECES = 3
 SORT_AHEAD = 1
 STORE_LAG = 0
@@ -30,6 +30,12 @@ ASSIST = ()
 MERGE_B = False
 LAST_A = True
 HEAD_Q_BANKS = True
+PAIR_B = False
+TAB_ON_ACT = False
+LAST_SPLIT = False
+FIRST_A = 12
+SORT_A = 2
+FIRST_ONE = 7
 
 
 def tile_paligemma2withexpertmodel_pa_kernel(
@@ -108,6 +114,7 @@ def tile_paligemma2withexpertmodel_pa_kernel(
         bank_turn = [0]
         head_t = [0]
         waiting = []
+        pair = {}
         loads_left = [True]
 
         def warm(count, name):
@@ -135,10 +142,17 @@ def tile_paligemma2withexpertmodel_pa_kernel(
                 words_of[(n, i)] = words[:, i * 512 : (i + 1) * 512]
             words_of[n] = words
 
+        def pieces_sorted(j):
+            if j >= FIRST_SORTED_JOB:
+                return SORTED_PIECES
+            if j >= FIRST_A:
+                return SORT_A
+            return 1 if j >= FIRST_ONE else 0
+
         def sort_words(j):
-            if j < FIRST_SORTED_JOB or j >= len(tjobs):
+            if pieces_sorted(j) == 0 or j >= len(tjobs):
                 return
-            n = SORTED_PIECES * 512
+            n = pieces_sorted(j) * 512
             sw = srt.tile([P, n], F32, name="sorted%d" % j, tag="sorted")
             nc.scalar.copy(
                 out=sw[:].rearrange("p (g u w) -> p g u w", u=2, w=P),
@@ -187,7 +201,7 @@ def tile_paligemma2withexpertmodel_pa_kernel(
                     banks[b] = tpp.tile([P, 2, 256], F32, name="tp%d_%d" % (j, b), tag="tp")
                     filled[b] = 0
                 for u in range(2):
-                    if j in sorted_words and i < SORTED_PIECES:
+                    if j in sorted_words and i < pieces_sorted(j):
                         off = i * 512 + g * 256
                         src = sorted_words[j][:, off + u * P : off + (u + 1) * P]
                     else:
@@ -262,6 +276,54 @@ def tile_paligemma2withexpertmodel_pa_kernel(
             x1 = x1.rearrange("p (h d) -> p h d", h=nh).unsqueeze(1).to_broadcast(shape)
             x2 = x2.rearrange("p (h d) -> p h d", h=nh).unsqueeze(1).to_broadcast(shape)
             pt = (m % 2) + (0 if st == "p" else 2)
+            if PAIR_B and form == "b":
+                q = m % 2
+                if q == 0:
+                    pair["a"] = ropep.tile([P, 2] + shape[1:], F32, name="t_a%d" % n, tag="t_a")
+                    pair["b"] = ropep.tile([P, 2] + shape[1:], F32, name="t_b%d" % n, tag="t_b")
+                nc.vector.tensor_tensor(
+                    out=pair["a"][:, q], in0=x1, in1=tab_a[:, pt].unsqueeze(2).to_broadcast(shape), op=MULT
+                )
+                nc.vector.tensor_tensor(
+                    out=pair["b"][:, q], in0=x2, in1=tab_b[:, pt].unsqueeze(2).to_broadcast(shape), op=MULT
+                )
+                if q == 1:
+                    o2 = outp.tile([P, 2, nh, 2, P], F32, name="o%d" % n, tag="o")
+                    nc.gpsimd.tensor_tensor(
+                        out=o2[:].rearrange("p q h f d -> p q f h d"), in0=pair["a"][:], in1=pair["b"][:], op=ADD
+                    )
+                    full = out_0 if s < 2 else out_1
+                    hs = (4 * s if s < 2 else 0) + h0
+                    dst2 = full[m // 2, (pt - 1) * P : (pt + 1) * P, hs : hs + nh, :]
+                    nc.sync.dma_start(
+                        out=dst2.rearrange("(q p) h d -> p q (h d)", p=P),
+                        in_=o2[:].rearrange("p q h f d -> p q (h f d)"),
+                    )
+                return
+            if LAST_SPLIT and form == "a" and n == len(units) - 1:
+                t_a = ropep.tile(shape, F32, name="t_a%d" % n, tag="t_a")
+                t_b = ropep.tile(shape, F32, name="t_b%d" % n, tag="t_b")
+                o = outp.tile([P, nh, 2, P], F32, name="o%d" % n, tag="o")
+                half = [P, 2, 2, P]
+                for q in range(2):
+                    hs = slice(2 * q, 2 * q + 2)
+                    nc.vector.tensor_tensor(
+                        out=t_a[:, :, hs, :], in0=x1[:, :, hs, :], in1=tab_a[:, pt].unsqueeze(2).to_broadcast(half), op=MULT
+                    )
+                    nc.vector.tensor_tensor(
+                        out=t_b[:, :, hs, :], in0=x2[:, :, hs, :], in1=tab_b[:, pt].unsqueeze(2).to_broadcast(half), op=MULT
+                    )
+                    adder = nc.gpsimd if q == 0 else nc.vector
+                    adder.tensor_tensor(
+                        out=o[:, hs].rearrange("p h f d -> p f h d"), in0=t_a[:, :, hs, :], in1=t_b[:, :, hs, :], op=ADD
+                    )
+                    full = out_0 if s < 2 else out_1
+                    h1 = (4 * s if s < 2 else 0) + 2 * q
+                    nc.sync.dma_start(
+                        out=full[m // 2, pt * P : (pt + 1) * P, h1 : h1 + 2, :].rearrange("p h d -> p (h d)"),
+                        in_=o[:, hs].rearrange("p h f d -> p (h f d)"),
+                    )
+                return
             t_a = ropep.tile(shape, F32, name="t_a%d" % n, tag="t_a")
             t_b = ropep.tile(shape, F32, name="t_b%d" % n, tag="t_b")
             nc.vector.tensor_tensor(
@@ -320,8 +382,12 @@ def tile_paligemma2withexpertmodel_pa_kernel(
         tjob(0)
         tjob(1)
         tjob(2)
-        nc.vector.tensor_scalar_mul(out=tab_b[:, :, 0, :], in0=tab_a[:, :, 1, :], scalar1=-1.0)
-        nc.vector.tensor_copy(out=tab_b[:, :, 1, :], in_=tab_a[:, :, 0, :])
+        if TAB_ON_ACT:
+            nc.scalar.mul(out=tab_b[:, :, 0, :], in_=tab_a[:, :, 1, :], mul=-1.0)
+            nc.scalar.copy(out=tab_b[:, :, 1, :], in_=tab_a[:, :, 0, :])
+        else:
+            nc.vector.tensor_scalar_mul(out=tab_b[:, :, 0, :], in0=tab_a[:, :, 1, :], scalar1=-1.0)
+            nc.vector.tensor_copy(out=tab_b[:, :, 1, :], in_=tab_a[:, :, 0, :])
         tjob(3)
         unit_mx(0)
         unit_mx(1)

@@ -30,7 +30,7 @@ ASSIST = ()
 MERGE_B = False
 LAST_A = True
 HEAD_Q_BANKS = True
-PAIR_B = False
+PAIR_B = True
 TAB_ON_ACT = False
 LAST_SPLIT = False
 FIRST_A = 12
@@ -279,18 +279,27 @@ def tile_paligemma2withexpertmodel_pa_kernel(
             if PAIR_B and form == "b":
                 q = m % 2
                 if q == 0:
-                    pair["a"] = ropep.tile([P, 2] + shape[1:], F32, name="t_a%d" % n, tag="t_a")
-                    pair["b"] = ropep.tile([P, 2] + shape[1:], F32, name="t_b%d" % n, tag="t_b")
+                    pair["a"] = ropep.tile([P, 2, nh, 2, P], F32, name="t_a%d" % n, tag="t_a")
+                    pair["b"] = ropep.tile([P, 2, nh, 2, P], F32, name="t_b%d" % n, tag="t_b")
                 nc.vector.tensor_tensor(
-                    out=pair["a"][:, q], in0=x1, in1=tab_a[:, pt].unsqueeze(2).to_broadcast(shape), op=MULT
+                    out=pair["a"][:, q].rearrange("p h f d -> p f h d"),
+                    in0=x1,
+                    in1=tab_a[:, pt].unsqueeze(2).to_broadcast(shape),
+                    op=MULT,
                 )
                 nc.vector.tensor_tensor(
-                    out=pair["b"][:, q], in0=x2, in1=tab_b[:, pt].unsqueeze(2).to_broadcast(shape), op=MULT
+                    out=pair["b"][:, q].rearrange("p h f d -> p f h d"),
+                    in0=x2,
+                    in1=tab_b[:, pt].unsqueeze(2).to_broadcast(shape),
+                    op=MULT,
                 )
                 if q == 1:
                     o2 = outp.tile([P, 2, nh, 2, P], F32, name="o%d" % n, tag="o")
                     nc.gpsimd.tensor_tensor(
-                        out=o2[:].rearrange("p q h f d -> p q f h d"), in0=pair["a"][:], in1=pair["b"][:], op=ADD
+                        out=o2[:].rearrange("p q h f d -> p (q h f d)"),
+                        in0=pair["a"][:].rearrange("p q h f d -> p (q h f d)"),
+                        in1=pair["b"][:].rearrange("p q h f d -> p (q h f d)"),
+                        op=ADD,
                     )
                     full = out_0 if s < 2 else out_1
                     hs = (4 * s if s < 2 else 0) + h0

@@ -36,6 +36,9 @@ LAST_SPLIT = False
 FIRST_A = 12
 SORT_A = 2
 FIRST_ONE = 7
+HEAD2 = False
+PAIR_ADDS_ON_V = 1
+TAB_ON_POOL = False
 
 
 def tile_paligemma2withexpertmodel_pa_kernel(
@@ -295,7 +298,8 @@ def tile_paligemma2withexpertmodel_pa_kernel(
                 )
                 if q == 1:
                     o2 = outp.tile([P, 2, nh, 2, P], F32, name="o%d" % n, tag="o")
-                    nc.gpsimd.tensor_tensor(
+                    pair_adder = nc.vector if n < 2 * PAIR_ADDS_ON_V else nc.gpsimd
+                    pair_adder.tensor_tensor(
                         out=o2[:].rearrange("p q h f d -> p (q h f d)"),
                         in0=pair["a"][:].rearrange("p q h f d -> p (q h f d)"),
                         in1=pair["b"][:].rearrange("p q h f d -> p (q h f d)"),
@@ -391,18 +395,29 @@ def tile_paligemma2withexpertmodel_pa_kernel(
         tjob(0)
         tjob(1)
         tjob(2)
-        if TAB_ON_ACT:
+        if TAB_ON_POOL:
+            nc.gpsimd.tensor_scalar(out=tab_b[:, :, 0, :], in0=tab_a[:, :, 1, :], scalar1=-1.0, scalar2=0.0, op0=MULT, op1=ADD)
+            nc.gpsimd.tensor_scalar(out=tab_b[:, :, 1, :], in0=tab_a[:, :, 0, :], scalar1=1.0, scalar2=0.0, op0=MULT, op1=ADD)
+        elif TAB_ON_ACT:
             nc.scalar.mul(out=tab_b[:, :, 0, :], in_=tab_a[:, :, 1, :], mul=-1.0)
             nc.scalar.copy(out=tab_b[:, :, 1, :], in_=tab_a[:, :, 0, :])
         else:
             nc.vector.tensor_scalar_mul(out=tab_b[:, :, 0, :], in0=tab_a[:, :, 1, :], scalar1=-1.0)
             nc.vector.tensor_copy(out=tab_b[:, :, 1, :], in_=tab_a[:, :, 0, :])
-        tjob(3)
-        unit_mx(0)
-        unit_mx(1)
-        unit_rope(0)
-        tjob(4)
-        unit_rope(1)
+        if HEAD2:
+            unit_mx(0)
+            unit_mx(1)
+            unit_rope(0)
+            tjob(3)
+            unit_rope(1)
+            tjob(4)
+        else:
+            tjob(3)
+            unit_mx(0)
+            unit_mx(1)
+            unit_rope(0)
+            tjob(4)
+            unit_rope(1)
         transposes(5, 0, 4)
         unit_mx(2)
         unit_mx(3)

@@ -17,7 +17,7 @@ P = 128
 RAW_BUFS = 7
 HEAD_JOBS = 6
 WARM_FIRST = 8
-WARM_TRANSPOSES = 24
+WARM_TRANSPOSES = 0
 FIRST_SORTED_JOB = 18
 SORTED_PIECES = 3
 SORT_AHEAD = 1
@@ -37,6 +37,12 @@ FIRST_A = 12
 SORT_A = 2
 FIRST_ONE = 7
 HEAD2 = False
+TAB_EARLY = False
+DEFER_Q3 = False
+HEAD_V_EVAC = False
+QA = 3
+QB = 15
+QSPLIT = 15
 PAIR_ADDS_ON_V = 1
 TAB_ON_POOL = False
 
@@ -212,11 +218,14 @@ def tile_paligemma2withexpertmodel_pa_kernel(
                     nc.tensor.transpose(banks[b][:, u, il * P : (il + 1) * P], src, ident[:])
                 filled[b] += 1
                 if filled[b] == 2:
-                    nc.scalar.copy(
+                    evac = nc.vector.tensor_copy if (HEAD_V_EVAC and j == 1 and b == 3) else nc.scalar.copy
+                    evac(
                         out=grouped[:, 256 * b : 256 * (b + 1), :].bitcast(F32),
                         in_=banks[b][:].rearrange("p u c -> p c u"),
                     )
-                    if j < HEAD_JOBS and (HEAD_Q_BANKS or nt == 1):
+                    if DEFER_Q3 and j == 3:
+                        pass
+                    elif j < HEAD_JOBS and (HEAD_Q_BANKS or nt == 1):
                         quantise(j, 256 * b, 256 * (b + 1))
                     elif j < HEAD_JOBS and len(filled) == nt and min(filled.values()) == 2:
                         quantise(j, 0, 256 * nt)
@@ -385,17 +394,28 @@ def tile_paligemma2withexpertmodel_pa_kernel(
 
         load(0)
         load(1)
-        load(2)
+        if not TAB_EARLY:
+            load(2)
         nc.sync.dma_start(out=tab_a[:, :, 0, :], in_=cos[0, :, 0, :].rearrange("(t p) d -> p t d", p=P))
         nc.sync.dma_start(out=tab_a[:, :, 1, :], in_=sin[0, :, 0, :].rearrange("(t p) d -> p t d", p=P))
+        if TAB_EARLY:
+            load(2)
         for n in range(3, HEAD_JOBS + RAW_BUFS):
             load(n)
         warm(WARM_FIRST, "scrap_first")
 
         tjob(0)
-        tjob(1)
+        if TAB_EARLY:
+            transposes(1, 0, 4)
+            nc.vector.tensor_scalar_mul(out=tab_b[:, :, 0, :], in0=tab_a[:, :, 1, :], scalar1=-1.0)
+            nc.vector.tensor_copy(out=tab_b[:, :, 1, :], in_=tab_a[:, :, 0, :])
+            transposes(1, 4, 4)
+        else:
+            tjob(1)
         tjob(2)
-        if TAB_ON_POOL:
+        if TAB_EARLY:
+            pass
+        elif TAB_ON_POOL:
             nc.gpsimd.tensor_scalar(out=tab_b[:, :, 0, :], in0=tab_a[:, :, 1, :], scalar1=-1.0, scalar2=0.0, op0=MULT, op1=ADD)
             nc.gpsimd.tensor_scalar(out=tab_b[:, :, 1, :], in0=tab_a[:, :, 0, :], scalar1=1.0, scalar2=0.0, op0=MULT, op1=ADD)
         elif TAB_ON_ACT:
@@ -416,6 +436,8 @@ def tile_paligemma2withexpertmodel_pa_kernel(
             unit_mx(0)
             unit_mx(1)
             unit_rope(0)
+            if DEFER_Q3:
+                quantise(3, 0, 256)
             tjob(4)
             unit_rope(1)
         transposes(5, 0, 4)
@@ -440,7 +462,7 @@ def tile_paligemma2withexpertmodel_pa_kernel(
                 load(jt + RAW_BUFS)
             if jt + RAW_BUFS >= len(tjobs) - 1:
                 loads_left[0] = False
-            quota = 4 * (j - 3) if j <= 15 else 48 + 8 * (j - 15)
+            quota = 4 * (j - QA) if j <= QSPLIT else 4 * (QSPLIT - QA) + 8 * (j - QB)
             if j == len(tjobs) - 1:
                 quota = 144
             while done < len(units) and issued < quota:

@@ -20,7 +20,7 @@ WARM_FIRST = 8
 WARM_TRANSPOSES = 0
 FIRST_SORTED_JOB = 18
 SORTED_PIECES = 3
-SORT_AHEAD = 1
+SORT_AHEAD = 2
 STORE_LAG = 0
 OUT_BUFS = 6
 ROPE_BUFS = 3
@@ -454,9 +454,9 @@ def tile_paligemma2withexpertmodel_pa_kernel(
             load(jt + RAW_BUFS)
         for j in range(HEAD_JOBS, len(tjobs)):
             jt = j + T_AHEAD
-            sort_words(jt + SORT_AHEAD)
             if jt < len(tjobs):
                 transposes(jt, 0, 8)
+            sort_words(jt + SORT_AHEAD)
             quantise(j, 0, 1024)
             if jt + RAW_BUFS < len(tjobs):
                 load(jt + RAW_BUFS)

@@ -21,8 +21,8 @@ WARM_TRANSPOSES = 0
 FIRST_SORTED_JOB = 18
 SORTED_PIECES = 3
 SORT_AHEAD = 2
-STORE_LAG = 0
-OUT_BUFS = 6
+STORE_LAG = 3
+OUT_BUFS = 8
 ROPE_BUFS = 3
 ADD_SPLIT = 1
 T_AHEAD = 1

from contextlib import ExitStack

import concourse.mybir as mybir
from concourse.masks import make_identity

F32 = mybir.dt.float32
BF16 = mybir.dt.bfloat16
U32 = mybir.dt.uint32
U8 = mybir.dt.uint8
E5X4 = mybir.dt.float8_e5m2_x4
MULT = mybir.AluOpType.mult
ADD = mybir.AluOpType.add

FLOPS = 2 * 512 * 3072 * (2048 + 1024)

P = 128
RAW_BUFS = 7
HEAD_JOBS = 6
WARM_FIRST = 8
WARM_TRANSPOSES = 0
FIRST_SORTED_JOB = 18
SORTED_PIECES = 3
SORT_AHEAD = 2
STORE_LAG = 3
OUT_BUFS = 8
ROPE_BUFS = 3
ADD_SPLIT = 1
T_AHEAD = 1
ASSIST = ()
MERGE_B = False
LAST_A = True
HEAD_Q_BANKS = True
PAIR_B = True
TAB_ON_ACT = False
LAST_SPLIT = False
FIRST_A = 12
SORT_A = 2
FIRST_ONE = 7
HEAD2 = False
TAB_EARLY = False
DEFER_Q3 = False
HEAD_V_EVAC = False
QA = 3
QB = 15
QSPLIT = 15
PAIR_ADDS_ON_V = 1
TAB_ON_POOL = False


def tile_paligemma2withexpertmodel_pa_kernel(
    tc, pg_embeds, exp_embeds, cos, sin, wq0, wk0, wq1, wk1, out_0, out_1
):
    nc = tc.nc
    xsrc = {"p": pg_embeds.flatten_outer_dims(), "e": exp_embeds.flatten_outer_dims()}
    wsrc = {"p": (wq0, wk0), "e": (wq1, wk1)}
    halves = {"p": 2, "e": 1}

    def w_rows(st, s):
        return (wsrc[st][0] if s < 2 else wsrc[st][1]), 1024 * (s % 2)

    def job_x(st, kh, m0, nt):
        src = xsrc[st][m0 * P : (m0 + nt) * P, kh * 1024 : (kh + 1) * 1024]
        return {"key": ("x", st, kh, m0), "kind": "x", "nt": nt, "place": list(range(nt)), "src": src}

    def job_a(st, s, f, kh):
        w, r0 = w_rows(st, s)
        src = w[r0 : r0 + 1024, kh * 1024 : (kh + 1) * 1024]
        view = src.rearrange("(h f p) k -> f p h k", f=2, p=P)[f]
        return {"key": ("a", st, s, f, kh), "kind": "w", "nt": 4, "place": [0, 1, 2, 3], "view": view}

    def job_b(st, s, hh, kh):
        w, r0 = w_rows(st, s)
        src = w[r0 + 512 * hh : r0 + 512 * (hh + 1), kh * 1024 : (kh + 1) * 1024]
        return {"key": ("b", st, s, hh, kh), "kind": "w", "nt": 4, "place": [0, 2, 1, 3], "src": src}

    def jobs_a(st, s):
        return [job_a(st, s, f, kh) for f in range(2) for kh in range(halves[st])]

    def jobs_b(st, s):
        return [job_b(st, s, hh, kh) for hh in range(2) for kh in range(halves[st])]

    tjobs = (
        [job_x("e", 0, 0, 1), job_b("e", 0, 0, 0), job_x("e", 0, 1, 1), job_x("e", 0, 2, 1), job_x("e", 0, 3, 1)]
        + [job_b("e", 0, 1, 0)]
        + jobs_a("e", 1) + jobs_a("e", 2)
        + [job_x("p", 0, 0, 4), job_x("p", 1, 0, 4)]
        + jobs_a("p", 0) + jobs_a("p", 1) + (jobs_a("p", 2) if LAST_A else jobs_b("p", 2))
    )
    units = (
        [("b", "e", 0, hh, m) for hh in range(2) for m in range(4)]
        + [("a", st, s, 0, m) for (st, s) in (("e", 1), ("e", 2), ("p", 0), ("p", 1)) for m in range(4)]
        + ([("a", "p", 2, 0, m) for m in range(4)] if LAST_A else [("b", "p", 2, hh, m) for hh in range(2) for m in range(4)])
    )

    with ExitStack() as ctx:
        ctx.enter_context(tc.manual_schedule())
        const = ctx.enter_context(tc.tile_pool(name="const", bufs=1))
        piecep = ctx.enter_context(tc.tile_pool(name="piecep", bufs=1))
        rawp = ctx.enter_context(tc.tile_pool(name="rawp", bufs=RAW_BUFS))
        grp = ctx.enter_context(tc.tile_pool(name="grp", bufs=3))
        srt = ctx.enter_context(tc.tile_pool(name="srt", bufs=3))
        wcp = ctx.enter_context(tc.tile_pool(name="wcp", bufs=8))
        xcp = ctx.enter_context(tc.tile_pool(name="xcp", bufs=1))
        ropep = ctx.enter_context(tc.tile_pool(name="ropep", bufs=ROPE_BUFS))
        outp = ctx.enter_context(tc.tile_pool(name="outp", bufs=OUT_BUFS))
        asp = ctx.enter_context(tc.tile_pool(name="asp", bufs=2))
        tpp = ctx.enter_context(tc.psum_pool(name="tpp", bufs=4))
        accp = ctx.enter_context(tc.psum_pool(name="accp", bufs=2))

        ident = const.tile([P, P], F32, name="ident", tag="ident")
        make_identity(nc, ident[:])
        tab_a = const.tile([P, 4, 2, P], BF16, name="tab_a", tag="tab_a")
        tab_b = const.tile([P, 4, 2, P], BF16, name="tab_b", tag="tab_b")

        zeros = const.tile([P, 512], BF16, name="zeros", tag="zeros")
        nc.vector.memset(zeros[:], 0.0)

        words_of = {}
        sorted_words = {}
        codes = {}
        state = {}
        accs = {}
        bank_turn = [0]
        head_t = [0]
        waiting = []
        pair = {}
        loads_left = [True]

        def warm(count, name):
            scrap = accp.tile([P, 512], F32, name=name, tag="acc0")
            for i in range(count):
                nc.tensor.matmul(scrap[:], lhsT=zeros[:, 0:P], rhs=zeros[:], start=True, stop=True)

        def piece_order(job):
            return sorted(range(job["nt"]), key=lambda i: job["place"][i])

        def load(n):
            job = tjobs[n]
            nt = job["nt"]
            if n < HEAD_JOBS:
                for i in piece_order(job):
                    pc = piecep.tile([P, 1024], BF16, name="pc%d_%d" % (n, i), tag="pc%d_%d" % (n, i))
                    nc.sync.dma_start(out=pc[:], in_=job["src"][i * P : (i + 1) * P, :])
                    words_of[(n, i)] = pc[:].bitcast(F32)
                return
            raw = rawp.tile([P, 4, 1024], BF16, name="raw%d" % n, tag="raw")
            view = job["view"] if "view" in job else job["src"].rearrange("(i p) k -> p i k", p=P)
            nc.sync.dma_start(out=raw[:], in_=view)
            words = raw[:].rearrange("p i k -> p (i k)").bitcast(F32)
            for i in range(nt):
                words_of[(n, i)] = words[:, i * 512 : (i + 1) * 512]
            words_of[n] = words

        def pieces_sorted(j):
            if j >= FIRST_SORTED_JOB:
                return SORTED_PIECES
            if j >= FIRST_A:
                return SORT_A
            return 1 if j >= FIRST_ONE else 0

        def sort_words(j):
            if pieces_sorted(j) == 0 or j >= len(tjobs):
                return
            n = pieces_sorted(j) * 512
            sw = srt.tile([P, n], F32, name="sorted%d" % j, tag="sorted")
            nc.scalar.copy(
                out=sw[:].rearrange("p (g u w) -> p g u w", u=2, w=P),
                in_=words_of[j][:, 0:n].rearrange("p (g w u) -> p g u w", w=P, u=2),
            )
            sorted_words[j] = sw

        def quantise(j, c0, c1):
            job = tjobs[j]
            nt = job["nt"]
            if job["key"] not in codes:
                if job["kind"] == "x":
                    cd = xcp.tile([P, 256 * nt], U32, name="xc%d" % j, tag="xc%d" % j, align_bytes=64)
                    sc = xcp.tile([P, 256 * nt], U8, name="xs%d" % j, tag="xs%d" % j, align_bytes=64)
                else:
                    cd = wcp.tile([P, 1024], U32, name="wc%d" % j, tag="wc", align_bytes=64)
                    sc = wcp.tile([P, 1024], U8, name="ws%d" % j, tag="ws", align_bytes=64)
                codes[job["key"]] = (cd, sc)
            grouped = state[j]["grouped"]
            cd, sc = codes[job["key"]]
            nc.vector.quantize_mx(
                out=cd[:, c0:c1].bitcast(E5X4),
                scales=sc[:, c0:c1],
                in_=grouped[:, c0:c1, :].rearrange("p c t -> p (c t)"),
            )

        def transposes(j, first, count):
            job = tjobs[j]
            nt = job["nt"]
            place = job["place"]
            if j not in state:
                grouped = grp.tile([P, 256 * nt, 4], BF16, name="grouped%d" % j, tag="grouped", align_bytes=64)
                state[j] = {"grouped": grouped, "banks": {}, "filled": {}}
            grouped = state[j]["grouped"]
            banks = state[j]["banks"]
            filled = state[j]["filled"]
            if j < HEAD_JOBS:
                order = [(i, g) for i in piece_order(job) for g in range(2)]
            else:
                order = [(place.index(cb % nt), cb // nt) for cb in range(2 * nt)]
            for (i, g) in order[first : first + count]:
                cb = g * nt + place[i]
                b = cb // 2
                il = cb % 2
                if b not in banks:
                    banks[b] = tpp.tile([P, 2, 256], F32, name="tp%d_%d" % (j, b), tag="tp")
                    filled[b] = 0
                for u in range(2):
                    if j in sorted_words and i < pieces_sorted(j):
                        off = i * 512 + g * 256
                        src = sorted_words[j][:, off + u * P : off + (u + 1) * P]
                    else:
                        src = words_of[(j, i)][:, g * 256 + u : (g + 1) * 256 : 2]
                    nc.tensor.transpose(banks[b][:, u, il * P : (il + 1) * P], src, ident[:])
                filled[b] += 1
                if filled[b] == 2:
                    evac = nc.vector.tensor_copy if (HEAD_V_EVAC and j == 1 and b == 3) else nc.scalar.copy
                    evac(
                        out=grouped[:, 256 * b : 256 * (b + 1), :].bitcast(F32),
                        in_=banks[b][:].rearrange("p u c -> p c u"),
                    )
                    if DEFER_Q3 and j == 3:
                        pass
                    elif j < HEAD_JOBS and (HEAD_Q_BANKS or nt == 1):
                        quantise(j, 256 * b, 256 * (b + 1))
                    elif j < HEAD_JOBS and len(filled) == nt and min(filled.values()) == 2:
                        quantise(j, 0, 256 * nt)
                if head_t[0] < WARM_TRANSPOSES:
                    head_t[0] += 2
                    if head_t[0] % 8 == 0:
                        warm(2, "scrap%d" % head_t[0])

        def tjob(j):
            nt = tjobs[j]["nt"]
            transposes(j, 0, 2 * nt)
            if j >= HEAD_JOBS:
                quantise(j, 0, 256 * nt)

        def x_operand(st, m, g):
            if st == "e":
                xc, xs = codes[("x", "e", 0, m)]
                c0 = g * P
            else:
                xc, xs = codes[("x", "p", g // 2, 0)]
                c0 = (g % 2) * 512 + m * P
            return xc[:, c0 : c0 + P].bitcast(E5X4), xs[:, c0 : c0 + P]

        def mx_group(acc, st, m, wkey):
            npass = 2 * halves[st]
            for g in range(npass):
                lhs, lhs_scale = x_operand(st, m, g)
                wc, ws = codes[wkey + (g // 2,)]
                c0 = (g % 2) * 512
                nc.tensor.matmul_mx(
                    out=acc[:],
                    lhsT=lhs,
                    lhsT_scale=lhs_scale,
                    rhs=wc[:, c0 : c0 + 512].bitcast(E5X4),
                    rhs_scale=ws[:, c0 : c0 + 512],
                    start=(g == 0),
                    stop=(g == npass - 1),
                )

        def unit_mx(n):
            form, st, s, hh, m = units[n]
            if form == "a":
                acc0 = accp.tile([P, 512], F32, name="acc%d_0" % n, tag="acc0")
                mx_group(acc0, st, m, ("a", st, s, 0))
                acc1 = accp.tile([P, 512], F32, name="acc%d_1" % n, tag="acc1")
                mx_group(acc1, st, m, ("a", st, s, 1))
                accs[n] = (acc0[:], acc1[:])
            else:
                acc = accp.tile([P, 512], F32, name="acc%d" % n, tag="acc%d" % (bank_turn[0] % 2))
                bank_turn[0] += 1
                mx_group(acc, st, m, ("b", st, s, hh))
                accs[n] = (acc[:, 0:256], acc[:, 256:512])

        def unit_rope(n):
            form, st, s, hh, m = units[n]
            nh = 4 if form == "a" else 2
            h0 = 0 if form == "a" else 2 * hh
            x1, x2 = accs[n]
            shape = [P, 2, nh, P]
            x1 = x1.rearrange("p (h d) -> p h d", h=nh).unsqueeze(1).to_broadcast(shape)
            x2 = x2.rearrange("p (h d) -> p h d", h=nh).unsqueeze(1).to_broadcast(shape)
            pt = (m % 2) + (0 if st == "p" else 2)
            if PAIR_B and form == "b":
                q = m % 2
                if q == 0:
                    pair["a"] = ropep.tile([P, 2, nh, 2, P], F32, name="t_a%d" % n, tag="t_a")
                    pair["b"] = ropep.tile([P, 2, nh, 2, P], F32, name="t_b%d" % n, tag="t_b")
                nc.vector.tensor_tensor(
                    out=pair["a"][:, q].rearrange("p h f d -> p f h d"),
                    in0=x1,
                    in1=tab_a[:, pt].unsqueeze(2).to_broadcast(shape),
                    op=MULT,
                )
                nc.vector.tensor_tensor(
                    out=pair["b"][:, q].rearrange("p h f d -> p f h d"),
                    in0=x2,
                    in1=tab_b[:, pt].unsqueeze(2).to_broadcast(shape),
                    op=MULT,
                )
                if q == 1:
                    o2 = outp.tile([P, 2, nh, 2, P], F32, name="o%d" % n, tag="o")
                    pair_adder = nc.vector if n < 2 * PAIR_ADDS_ON_V else nc.gpsimd
                    pair_adder.tensor_tensor(
                        out=o2[:].rearrange("p q h f d -> p (q h f d)"),
                        in0=pair["a"][:].rearrange("p q h f d -> p (q h f d)"),
                        in1=pair["b"][:].rearrange("p q h f d -> p (q h f d)"),
                        op=ADD,
                    )
                    full = out_0 if s < 2 else out_1
                    hs = (4 * s if s < 2 else 0) + h0
                    dst2 = full[m // 2, (pt - 1) * P : (pt + 1) * P, hs : hs + nh, :]
                    nc.sync.dma_start(
                        out=dst2.rearrange("(q p) h d -> p q (h d)", p=P),
                        in_=o2[:].rearrange("p q h f d -> p q (h f d)"),
                    )
                return
            if LAST_SPLIT and form == "a" and n == len(units) - 1:
                t_a = ropep.tile(shape, F32, name="t_a%d" % n, tag="t_a")
                t_b = ropep.tile(shape, F32, name="t_b%d" % n, tag="t_b")
                o = outp.tile([P, nh, 2, P], F32, name="o%d" % n, tag="o")
                half = [P, 2, 2, P]
                for q in range(2):
                    hs = slice(2 * q, 2 * q + 2)
                    nc.vector.tensor_tensor(
                        out=t_a[:, :, hs, :], in0=x1[:, :, hs, :], in1=tab_a[:, pt].unsqueeze(2).to_broadcast(half), op=MULT
                    )
                    nc.vector.tensor_tensor(
                        out=t_b[:, :, hs, :], in0=x2[:, :, hs, :], in1=tab_b[:, pt].unsqueeze(2).to_broadcast(half), op=MULT
                    )
                    adder = nc.gpsimd if q == 0 else nc.vector
                    adder.tensor_tensor(
                        out=o[:, hs].rearrange("p h f d -> p f h d"), in0=t_a[:, :, hs, :], in1=t_b[:, :, hs, :], op=ADD
                    )
                    full = out_0 if s < 2 else out_1
                    h1 = (4 * s if s < 2 else 0) + 2 * q
                    nc.sync.dma_start(
                        out=full[m // 2, pt * P : (pt + 1) * P, h1 : h1 + 2, :].rearrange("p h d -> p (h d)"),
                        in_=o[:, hs].rearrange("p h f d -> p (h f d)"),
                    )
                return
            t_a = ropep.tile(shape, F32, name="t_a%d" % n, tag="t_a")
            t_b = ropep.tile(shape, F32, name="t_b%d" % n, tag="t_b")
            nc.vector.tensor_tensor(
                out=t_a[:], in0=x1, in1=tab_a[:, pt].unsqueeze(2).to_broadcast(shape), op=MULT
            )
            if n in ASSIST:
                xs = asp.tile([P, nh, P], F32, name="xs%d" % n, tag="xs")
                nc.scalar.copy(out=xs[:], in_=accs[n][1].rearrange("p (h d) -> p h d", h=nh))
                nc.gpsimd.tensor_tensor(
                    out=t_b[:], in0=xs[:].unsqueeze(1).to_broadcast(shape), in1=tab_b[:, pt].unsqueeze(2).to_broadcast(shape), op=MULT
                )
            else:
                nc.vector.tensor_tensor(
                    out=t_b[:], in0=x2, in1=tab_b[:, pt].unsqueeze(2).to_broadcast(shape), op=MULT
                )
            o = outp.tile([P, nh, 2, P], F32, name="o%d" % n, tag="o")
            adder = nc.vector if n == len(units) - 1 else nc.gpsimd
            parts = ADD_SPLIT if (form == "a" and adder is nc.gpsimd) else 1
            hp = nh // parts
            for q in range(parts):
                adder.tensor_tensor(
                    out=o[:, q * hp : (q + 1) * hp].rearrange("p h f d -> p f h d"),
                    in0=t_a[:, :, q * hp : (q + 1) * hp, :],
                    in1=t_b[:, :, q * hp : (q + 1) * hp, :],
                    op=ADD,
                )
            b = m // 2
            rows = slice(pt * P, (pt + 1) * P)
            if s < 2:
                dst = out_0[b, rows, 4 * s + h0 : 4 * s + h0 + nh, :]
            else:
                dst = out_1[b, rows, h0 : h0 + nh, :]
            waiting.append((dst, o))
            while len(waiting) > (STORE_LAG if loads_left[0] else 0):
                store()

        def store():
            dst, o = waiting.pop(0)
            nc.sync.dma_start(
                out=dst.rearrange("p h d -> p (h d)"),
                in_=o[:].rearrange("p h f d -> p (h f d)"),
            )

        def passes_of(n):
            return (4 if units[n][0] == "a" else 2) * halves[units[n][1]]

        load(0)
        load(1)
        if not TAB_EARLY:
            load(2)
        nc.sync.dma_start(out=tab_a[:, :, 0, :], in_=cos[0, :, 0, :].rearrange("(t p) d -> p t d", p=P))
        nc.sync.dma_start(out=tab_a[:, :, 1, :], in_=sin[0, :, 0, :].rearrange("(t p) d -> p t d", p=P))
        if TAB_EARLY:
            load(2)
        for n in range(3, HEAD_JOBS + RAW_BUFS):
            load(n)
        warm(WARM_FIRST, "scrap_first")

        tjob(0)
        if TAB_EARLY:
            transposes(1, 0, 4)
            nc.vector.tensor_scalar_mul(out=tab_b[:, :, 0, :], in0=tab_a[:, :, 1, :], scalar1=-1.0)
            nc.vector.tensor_copy(out=tab_b[:, :, 1, :], in_=tab_a[:, :, 0, :])
            transposes(1, 4, 4)
        else:
            tjob(1)
        tjob(2)
        if TAB_EARLY:
            pass
        elif TAB_ON_POOL:
            nc.gpsimd.tensor_scalar(out=tab_b[:, :, 0, :], in0=tab_a[:, :, 1, :], scalar1=-1.0, scalar2=0.0, op0=MULT, op1=ADD)
            nc.gpsimd.tensor_scalar(out=tab_b[:, :, 1, :], in0=tab_a[:, :, 0, :], scalar1=1.0, scalar2=0.0, op0=MULT, op1=ADD)
        elif TAB_ON_ACT:
            nc.scalar.mul(out=tab_b[:, :, 0, :], in_=tab_a[:, :, 1, :], mul=-1.0)
            nc.scalar.copy(out=tab_b[:, :, 1, :], in_=tab_a[:, :, 0, :])
        else:
            nc.vector.tensor_scalar_mul(out=tab_b[:, :, 0, :], in0=tab_a[:, :, 1, :], scalar1=-1.0)
            nc.vector.tensor_copy(out=tab_b[:, :, 1, :], in_=tab_a[:, :, 0, :])
        if HEAD2:
            unit_mx(0)
            unit_mx(1)
            unit_rope(0)
            tjob(3)
            unit_rope(1)
            tjob(4)
        else:
            tjob(3)
            unit_mx(0)
            unit_mx(1)
            unit_rope(0)
            if DEFER_Q3:
                quantise(3, 0, 256)
            tjob(4)
            unit_rope(1)
        transposes(5, 0, 4)
        unit_mx(2)
        unit_mx(3)
        unit_rope(2)
        transposes(5, 4, 4)
        unit_rope(3)

        done = 4
        issued = 8
        for jt in range(HEAD_JOBS, HEAD_JOBS + T_AHEAD):
            transposes(jt, 0, 8)
            load(jt + RAW_BUFS)
        for j in range(HEAD_JOBS, len(tjobs)):
            jt = j + T_AHEAD
            if jt < len(tjobs):
                transposes(jt, 0, 8)
            sort_words(jt + SORT_AHEAD)
            quantise(j, 0, 1024)
            if jt + RAW_BUFS < len(tjobs):
                load(jt + RAW_BUFS)
            if jt + RAW_BUFS >= len(tjobs) - 1:
                loads_left[0] = False
            quota = 4 * (j - QA) if j <= QSPLIT else 4 * (QSPLIT - QA) + 8 * (j - QB)
            if j == len(tjobs) - 1:
                quota = 144
            while done < len(units) and issued < quota:
                issued += passes_of(done)
                unit_mx(done)
                unit_rope(done)
                done += 1
